import numpy as np
import ml_dtypes


def mxq(x, axis, fmt="e4m3"):
    dtype, down = {"e4m3": (ml_dtypes.float8_e4m3fn, 7), "e5m2": (ml_dtypes.float8_e5m2, 14)}[fmt]
    v = np.moveaxis(np.asarray(x, np.float32).astype(ml_dtypes.bfloat16).astype(np.float64), axis, -1)
    blocks = v.reshape(v.shape[:-1] + (-1, 32))
    amax = np.abs(blocks).max(-1, keepdims=True)
    byte = np.maximum(np.where(amax > 0, np.frexp(amax)[1] - 1 + 127, 0) - down, 1)
    scale = np.exp2(byte - 127.0)
    codes = (blocks / scale).astype(np.float32).astype(dtype).astype(np.float64)
    return np.moveaxis((codes * scale).reshape(v.shape), -1, axis)


WIDE = False


def mx_kscale(k):
    if not WIDE:
        return np.ones(k)
    levels = np.array([10, -10, 5, -5, 0])
    a = np.random.permutation(np.resize(levels, k // 512 * 4)).reshape(k // 512, 4)
    idx = np.arange(k)
    return np.exp2(a[idx // 512, idx % 128 // 32])


BF16 = ml_dtypes.bfloat16


def bf(x):
    return np.asarray(x, np.float32).astype(BF16)


def f64(x):
    return np.asarray(x).astype(np.float64)


E2M1 = np.array([0.0, 0.5, 1.0, 1.5, 2.0, 3.0, 4.0, 6.0, -0.0, -0.5, -1.0, -1.5, -2.0, -3.0, -4.0, -6.0])


def pack_weight(w, fmt):
    k, n = w.shape
    w = f64(bf(w)).reshape(k // 32, 32, n)
    amax = np.abs(w).max(1)
    if fmt == "e4m3":
        byte = np.frexp(amax)[1] - 1 + 127 - 7
    else:
        mant, ex = np.frexp(amax / 6.0)
        byte = np.where(mant > 0.5, ex, ex - 1) + 127
    byte = np.clip(np.where(amax > 0, byte, 1), 1, 254)
    scaled = (w * np.exp2(127.0 - byte)[:, None, :]).reshape(k, n).astype(np.float32)
    by_word = np.ascontiguousarray(scaled.reshape(k // 512, 128, 4, n).transpose(0, 1, 3, 2))
    if fmt == "e4m3":
        words = by_word.astype(ml_dtypes.float8_e4m3fn).view(np.uint8)
    else:
        c = by_word.astype(ml_dtypes.float4_e2m1fn).view(np.uint8) & 0xF
        words = c[..., 0::2] | (c[..., 1::2] << 4)
    return np.ascontiguousarray(words), np.ascontiguousarray(byte.astype(np.uint8).reshape(k // 512, 16, n))


def unpack_weight(words, scales, fmt):
    g, p, n, _ = words.shape
    if fmt == "e4m3":
        vals = np.ascontiguousarray(words).view(ml_dtypes.float8_e4m3fn).astype(np.float64)
    else:
        nib = np.empty((g, p, n, 4), np.uint8)
        nib[..., 0::2] = words & 0xF
        nib[..., 1::2] = words >> 4
        vals = E2M1[nib]
    vals = vals * np.repeat(np.exp2(scales.astype(np.float64) - 127.0), 8, axis=1)[..., None]
    return vals.transpose(0, 1, 3, 2).reshape(g * 512, n)


B, N, F_IN, D_OUT, EMB_DIM, H1 = 1, 1024, 8192, 128, 16, 4
NEG_INF = -1e9
LN_EPS = 1e-3


def setup_inputs():
    r = np.random.standard_normal
    s = mx_kscale(F_IN)
    adj = (0.3 + 0.4 * np.random.random_sample((N, N))) * (np.random.random_sample((N, N)) < 0.5)
    np.fill_diagonal(adj, 1.0)
    q2 = bf(r((B, N, D_OUT)) * 1.6)
    k2 = bf(r((B, N, D_OUT)) * 1.6)
    v2 = bf(r((B, N, D_OUT)) * 0.2)
    adj = bf(adj)
    x = bf(r((B, N, F_IN)) * s)
    proj_w_words, proj_w_scales = pack_weight(r((F_IN, D_OUT)) * 0.1 / np.sqrt(F_IN) / s[:, None], "e4m3")
    ln_g = bf(1.0 + 0.1 * r(D_OUT))
    ln_b = bf(0.1 * r(D_OUT))
    return {"q2": q2, "k2": k2, "v2": v2,
            "adj": adj,
            "x": x, "proj_w_words": proj_w_words, "proj_w_scales": proj_w_scales,
            "ln_g": ln_g, "ln_b": ln_b}


def reference(q2, k2, v2, adj, x, proj_w_words, proj_w_scales, ln_g, ln_b):
    scores = f64(q2) @ f64(k2).transpose(0, 2, 1) / np.sqrt(D_OUT)
    scores = np.where(f64(adj)[None] == 0, NEG_INF, scores)
    e = np.exp(scores - scores.max(-1, keepdims=True))
    h = (mxq(e, 2, "e4m3") @ mxq(f64(v2), 1, "e4m3")) / e.sum(-1, keepdims=True)
    skip = mxq(f64(x), 2, "e4m3") @ unpack_weight(proj_w_words, proj_w_scales, "e4m3")
    y = h + skip
    mu = y.mean(-1, keepdims=True)
    var = ((y - mu) ** 2).mean(-1, keepdims=True)
    return (y - mu) / np.sqrt(var + LN_EPS) * f64(ln_g) + f64(ln_b)

@@ -1,0 +1,330 @@
+from contextlib import ExitStack
+import math
+
+import concourse.masks as masks
+import concourse.mybir as mybir
+
+F32 = mybir.dt.float32
+BF16 = mybir.dt.bfloat16
+I32 = mybir.dt.int32
+U32 = mybir.dt.uint32
+U8 = mybir.dt.uint8
+FP8X4 = mybir.dt.float8_e4m3fn_x4
+ALU = mybir.AluOpType
+ACT = mybir.ActivationFunctionType
+AXIS_X = mybir.AxisListType.X
+
+P = 128
+PACK = 4
+K_PASS = P * PACK
+NODES = 1024
+D = 128
+F_IN = 8192
+TILES = NODES // P
+KEY_PASSES = NODES // K_PASS
+SKIP_PASSES = F_IN // K_PASS
+BANK = 512
+SCORE_HALVES = NODES // BANK
+
+CHUNK_PASSES = 4
+CHUNK_K = CHUNK_PASSES * K_PASS
+CHUNKS_PER_TILE = F_IN // CHUNK_K
+CHUNKS = TILES * CHUNKS_PER_TILE
+ROUND_CHUNKS = 2
+ROUNDS = CHUNKS // ROUND_CHUNKS
+ROUNDS_PER_TILE = ROUNDS // TILES
+LOAD_AHEAD = 12
+
+SCALE = 1.0 / math.sqrt(D)
+NEG_INF = -1e9
+LN_EPS = 1e-3
+
+FLOPS = 2 * NODES * NODES * D * 2 + 2 * NODES * F_IN * D
+
+
+def tile_spatialprocessor_pa_k_kernel(
+    tc, q2, k2, v2, adj, x, proj_w_words, proj_w_scales, ln_g, ln_b, out
+):
+    nc = tc.nc
+    x_rows = x.rearrange("b n k -> (b n) k")
+    out_rows = out.rearrange("b n d -> (b n) d")
+
+    with ExitStack() as ctx:
+        ctx.enter_context(tc.manual_schedule())
+        keep = ctx.enter_context(tc.tile_pool(name="keep", bufs=1))
+        x_pool = ctx.enter_context(tc.tile_pool(name="x", bufs=LOAD_AHEAD * ROUND_CHUNKS))
+        adj_pool = ctx.enter_context(tc.tile_pool(name="adj", bufs=TILES))
+        grouped_pool = ctx.enter_context(tc.tile_pool(name="grouped", bufs=4))
+        code_pool = ctx.enter_context(tc.tile_pool(name="codes", bufs=6))
+        att_pool = ctx.enter_context(tc.tile_pool(name="attention", bufs=2))
+        column_pool = ctx.enter_context(tc.tile_pool(name="columns", bufs=4))
+        norm_pool = ctx.enter_context(tc.tile_pool(name="norm", bufs=3))
+        flip_psum = ctx.enter_context(tc.psum_pool(name="flip", bufs=4))
+        score_psum = ctx.enter_context(tc.psum_pool(name="score", bufs=2))
+        skip_psum = ctx.enter_context(tc.psum_pool(name="skip", bufs=2))
+
+        w_planes = keep.tile([P, SKIP_PASSES, D], U8, align_bytes=64)
+        nc.vector.memset(w_planes[:].bitcast(I32), 0)
+        neg_half = keep.tile([P, 1], F32)
+        nc.vector.memset(neg_half[:], -0.5)
+        table_warm = keep.tile([P, 1], F32)
+        nc.scalar.activation(out=table_warm[:], in_=neg_half[:], func=ACT.Exp)
+        ident_bf = keep.tile([P, P], BF16)
+        masks.make_identity(nc, ident_bf[:])
+        ident_f32 = keep.tile([P, P], F32)
+        masks.make_identity(nc, ident_f32[:])
+
+        q_rows = keep.tile([P, TILES, D], BF16)
+        k_rows = keep.tile([P, TILES, D], BF16)
+        v_rows = keep.tile([P, TILES, D], BF16)
+        nc.sync.dma_start(out=q_rows[:], in_=q2.rearrange("b (t p) d -> p (b t) d", p=P))
+        nc.sync.dma_start(out=k_rows[:], in_=k2.rearrange("b (t p) d -> p (b t) d", p=P))
+        nc.sync.dma_start(out=v_rows[:], in_=v2.rearrange("b (t p) d -> p (b t) d", p=P))
+
+        adj_tiles = []
+        x_chunks = []
+
+        def load_adj_tile():
+            a = len(adj_tiles)
+            adj_tile = adj_pool.tile([P, NODES], BF16, name="adj_tile")
+            nc.sync.dma_start(out=adj_tile[:], in_=adj[P * a : P * (a + 1), :])
+            adj_tiles.append(adj_tile)
+
+        def load_round(n):
+            for c in range(ROUND_CHUNKS * n, ROUND_CHUNKS * (n + 1)):
+                r, part = divmod(c, CHUNKS_PER_TILE)
+                x_chunk = x_pool.tile([P, CHUNK_K], BF16, name="x_chunk")
+                nc.sync.dma_start(
+                    out=x_chunk[:],
+                    in_=x_rows[P * r : P * (r + 1), CHUNK_K * part : CHUNK_K * (part + 1)],
+                )
+                x_chunks.append(x_chunk)
+            if n % ROUNDS_PER_TILE == 0 and len(adj_tiles) < TILES:
+                load_adj_tile()
+
+        load_adj_tile()
+        load_round(0)
+        load_round(1)
+        w_scale_words = proj_w_scales.bitcast(I32)
+        for quadrant in range(4):
+            nc.sync.dma_start(
+                out=w_planes[32 * quadrant : 32 * quadrant + 4, :, :].bitcast(I32),
+                in_=w_scale_words[:, 4 * quadrant : 4 * quadrant + 4, :].rearrange("g r n -> r g n"),
+            )
+        w_codes = keep.tile([P, SKIP_PASSES, D], U32, align_bytes=64)
+        nc.sync.dma_start(
+            out=w_codes[:].bitcast(I32),
+            in_=proj_w_words.bitcast(I32).rearrange("g p n o -> p g (n o)"),
+        )
+        gain = keep.tile([P, D], BF16)
+        shift = keep.tile([P, D], BF16)
+        nc.sync.dma_start(out=gain[:], in_=ln_g.partition_broadcast(P))
+        nc.sync.dma_start(out=shift[:], in_=ln_b.partition_broadcast(P))
+        for n in range(2, LOAD_AHEAD):
+            load_round(n)
+
+        def flip_rows(rows, name):
+            bank = flip_psum.tile([P, TILES, P], BF16, name="qk_bank", tag="flip")
+            for t in range(TILES):
+                nc.tensor.transpose(bank[:, t, :], rows[:, t, :], ident_bf[:])
+            columns = keep.tile([P, NODES], BF16, name=name)
+            nc.scalar.copy(out=columns[:], in_=bank[:].rearrange("d t i -> d (t i)"))
+            return columns
+
+        q_cols = flip_rows(q_rows, "q_cols")
+        k_cols = flip_rows(k_rows, "k_cols")
+
+        v_grouped = keep.tile([P, KEY_PASSES, D, PACK], BF16, align_bytes=64)
+        for c in range(KEY_PASSES):
+            nc.vector.tensor_copy(
+                out=v_grouped[:, c],
+                in_=v_rows[:, PACK * c : PACK * (c + 1), :].rearrange("p t d -> p d t"),
+            )
+        v_codes = keep.tile([P, KEY_PASSES * D], U32, align_bytes=64)
+        v_planes = keep.tile([P, KEY_PASSES * D], U8, align_bytes=64)
+        nc.vector.quantize_mx(
+            out=v_codes[:].bitcast(FP8X4),
+            scales=v_planes[:],
+            in_=v_grouped[:].rearrange("p c d t -> p (c d t)"),
+        )
+
+        masked = {}
+        e_rows = {}
+        row_sums = {}
+        e_grouped = {}
+        e_operands = {}
+        h_rows = {}
+
+        def scores(m):
+            a, half = divmod(m, SCORE_HALVES)
+            if half == 0:
+                nc.vector.tensor_scalar(
+                    out=adj_tiles[a][:], in0=adj_tiles[a][:],
+                    scalar1=0.0, scalar2=NEG_INF, op0=ALU.is_equal, op1=ALU.mult,
+                )
+                masked[a] = att_pool.tile([P, NODES], F32, name="masked")
+            keys = slice(BANK * half, BANK * (half + 1))
+            bank = score_psum.tile([P, BANK], F32, name="score_bank", tag="score")
+            nc.tensor.matmul(
+                out=bank[:], lhsT=q_cols[:, P * a : P * (a + 1)], rhs=k_cols[:, keys], start=True, stop=True
+            )
+            nc.vector.scalar_tensor_tensor(
+                out=masked[a][:, keys], in0=bank[:], scalar=SCALE, in1=adj_tiles[a][:, keys],
+                op0=ALU.mult, op1=ALU.add,
+            )
+
+        def softmax(a):
+            neg_max = column_pool.tile([P, 1], F32, name="neg_max")
+            nc.vector.tensor_reduce(out=neg_max[:], in_=masked[a][:], axis=AXIS_X, op=ALU.max, negate=True)
+            e_rows[a] = att_pool.tile([P, NODES], BF16, name="e_rows")
+            row_sums[a] = column_pool.tile([P, 1], F32, name="row_sum")
+            nc.scalar.activation(
+                out=e_rows[a][:], in_=masked[a][:], func=ACT.Exp, bias=neg_max[:], scale=1.0,
+                accum_out=row_sums[a][:],
+            )
+
+        def flip_e(a):
+            bank = flip_psum.tile([P, TILES, P], BF16, name="e_bank", tag="flip")
+            for s in range(TILES):
+                nc.tensor.transpose(bank[:, s, :], e_rows[a][:, P * s : P * (s + 1)], ident_bf[:])
+            e_grouped[a] = att_pool.tile([P, KEY_PASSES, P, PACK], BF16, name="e_grouped", align_bytes=64)
+            nc.scalar.copy(out=e_grouped[a][:], in_=bank[:].rearrange("p (c t) i -> p c i t", t=PACK))
+
+        def quantise_e(a):
+            codes = att_pool.tile([P, KEY_PASSES * P], U32, name="e_codes", align_bytes=64)
+            planes = att_pool.tile([P, KEY_PASSES * P], U8, name="e_planes", align_bytes=64)
+            nc.vector.quantize_mx(
+                out=codes[:].bitcast(FP8X4), scales=planes[:],
+                in_=e_grouped[a][:].rearrange("p c i t -> p (c i t)"),
+            )
+            inv_sum = column_pool.tile([P, 1], F32, name="inv_sum")
+            nc.vector.reciprocal(out=inv_sum[:], in_=row_sums[a][:])
+            e_operands[a] = (codes, planes, inv_sum)
+
+        def weighted_values(a):
+            codes, planes, inv_sum = e_operands[a]
+            bank = score_psum.tile([P, D], F32, name="h_bank", tag="score")
+            for c in range(KEY_PASSES):
+                nc.tensor.matmul_mx(
+                    out=bank[:],
+                    lhsT=codes[:, P * c : P * (c + 1)].bitcast(FP8X4),
+                    lhsT_scale=planes[:, P * c : P * (c + 1)],
+                    rhs=v_codes[:, D * c : D * (c + 1)].bitcast(FP8X4),
+                    rhs_scale=v_planes[:, D * c : D * (c + 1)],
+                    start=(c == 0),
+                    stop=(c == KEY_PASSES - 1),
+                )
+            h_rows[a] = norm_pool.tile([P, D], F32, name="h_rows")
+            nc.vector.tensor_scalar(
+                out=h_rows[a][:], in0=bank[:], scalar1=inv_sum[:], scalar2=None, op0=ALU.mult
+            )
+
+        x_grouped = {}
+        x_operands = {}
+        skip_banks = {}
+
+        def flip_x(c):
+            words = x_chunks[c][:].bitcast(F32)
+            x_grouped[c] = grouped_pool.tile([P, CHUNK_PASSES, P, PACK], BF16, name="x_grouped", align_bytes=64)
+            grouped_words = x_grouped[c][:].bitcast(F32)
+            for first in range(0, CHUNK_PASSES, 2):
+                bank = flip_psum.tile([P, 2, 2, P], F32, name="x_bank", tag="flip")
+                for g in range(2):
+                    start_word = (K_PASS // 2) * (first + g)
+                    for u in range(2):
+                        nc.tensor.transpose(
+                            bank[:, g, u, :],
+                            words[:, start_word + u : start_word + K_PASS // 2 : 2],
+                            ident_f32[:],
+                        )
+                nc.scalar.copy(
+                    out=grouped_words[:, first : first + 2], in_=bank[:].rearrange("p g u n -> p g n u")
+                )
+
+        def quantise_x(c):
+            codes = code_pool.tile([P, CHUNK_PASSES * P], U32, name="x_codes", align_bytes=64)
+            planes = code_pool.tile([P, CHUNK_PASSES * P], U8, name="x_planes", align_bytes=64)
+            nc.vector.quantize_mx(
+                out=codes[:].bitcast(FP8X4), scales=planes[:],
+                in_=x_grouped[c][:].rearrange("p g n t -> p (g n t)"),
+            )
+            x_operands[c] = (codes, planes)
+
+        def skip_passes(c):
+            r, part = divmod(c, CHUNKS_PER_TILE)
+            if part == 0:
+                skip_banks[r] = skip_psum.tile([P, D], F32, name="skip_bank", tag="skip")
+            codes, planes = x_operands[c]
+            for g in range(CHUNK_PASSES):
+                w_pass = CHUNK_PASSES * part + g
+                nc.tensor.matmul_mx(
+                    out=skip_banks[r][:],
+                    lhsT=codes[:, P * g : P * (g + 1)].bitcast(FP8X4),
+                    lhsT_scale=planes[:, P * g : P * (g + 1)],
+                    rhs=w_codes[:, w_pass, :].bitcast(FP8X4),
+                    rhs_scale=w_planes[:, w_pass, :],
+                    start=(w_pass == 0),
+                    stop=(w_pass == SKIP_PASSES - 1),
+                )
+
+        centred = {}
+        inv_std = {}
+
+        def norm_statistics(r):
+            y = norm_pool.tile([P, D], F32, name="y")
+            nc.vector.tensor_tensor(out=y[:], in0=skip_banks[r][:], in1=h_rows[r][:], op=ALU.add)
+            stats = column_pool.tile([P, 6], F32, name="stats")
+            nc.vector.bn_stats(out=stats[:], in_=y[:])
+            mean_var = column_pool.tile([P, 2], F32, name="mean_var")
+            nc.vector.bn_aggr(out=mean_var[:], in_=stats[:])
+            var_eps = column_pool.tile([P, 1], F32, name="var_eps")
+            nc.gpsimd.tensor_scalar(
+                out=var_eps[:], in0=mean_var[:, 1:2], scalar1=LN_EPS, scalar2=None, op0=ALU.add
+            )
+            inv_std[r] = column_pool.tile([P, 1], F32, name="inv_std")
+            nc.gpsimd.tensor_tensor(out=inv_std[r][:], in0=var_eps[:], in1=neg_half[:], op=ALU.pow)
+            centred[r] = norm_pool.tile([P, D], F32, name="centred")
+            nc.vector.scalar_tensor_tensor(
+                out=centred[r][:], in0=y[:], scalar=mean_var[:, 0:1], in1=gain[:],
+                op0=ALU.subtract, op1=ALU.mult,
+            )
+
+        def norm_finish(r):
+            result = norm_pool.tile([P, D], F32, name="result")
+            nc.vector.scalar_tensor_tensor(
+                out=result[:], in0=centred[r][:], scalar=inv_std[r][:], in1=shift[:],
+                op0=ALU.mult, op1=ALU.add,
+            )
+            nc.sync.dma_start(out=out_rows[P * r : P * (r + 1), :], in_=result[:])
+
+        scores_issued = 0
+        for n in range(ROUNDS + 1):
+            first_of_tile = n % ROUNDS_PER_TILE == 0
+            closing = n // ROUNDS_PER_TILE - 1
+            if not first_of_tile and closing >= 0:
+                norm_finish(closing)
+            if n < ROUNDS:
+                flip_x(ROUND_CHUNKS * n)
+                scores_due = min(n + 2, TILES * SCORE_HALVES)
+                for m in range(scores_issued, scores_due):
+                    scores(m)
+                scores_issued = scores_due
+                flip_x(ROUND_CHUNKS * n + 1)
+                if n + LOAD_AHEAD < ROUNDS:
+                    load_round(n + LOAD_AHEAD)
+                if first_of_tile:
+                    softmax(n // ROUNDS_PER_TILE)
+                else:
+                    flip_e(n // ROUNDS_PER_TILE)
+                quantise_x(ROUND_CHUNKS * n)
+                quantise_x(ROUND_CHUNKS * n + 1)
+                if not first_of_tile:
+                    quantise_e(n // ROUNDS_PER_TILE)
+            if first_of_tile and closing >= 0:
+                weighted_values(closing)
+            if n >= 1:
+                skip_passes(ROUND_CHUNKS * (n - 1))
+                skip_passes(ROUND_CHUNKS * (n - 1) + 1)
+            if first_of_tile and closing >= 0:
+                norm_statistics(closing)
+        norm_finish(TILES - 1)

@@ -37,6 +37,7 @@ LOAD_AHEAD = 12
 
 SCALE = 1.0 / math.sqrt(D)
 NEG_INF = -1e9
+PENALTY = -NEG_INF / SCALE
 LN_EPS = 1e-3
 
 FLOPS = 2 * NODES * NODES * D * 2 + 2 * NODES * F_IN * D
@@ -46,16 +47,17 @@ def tile_spatialprocessor_pa_k_kernel(
     tc, q2, k2, v2, adj, x, proj_w_words, proj_w_scales, ln_g, ln_b, out
 ):
     nc = tc.nc
-    x_rows = x.rearrange("b n k -> (b n) k")
-    out_rows = out.rearrange("b n d -> (b n) d")
+    x_tiles = x.rearrange("b (p t) k -> (b t) p k", t=TILES)
+    adj_rows = adj.rearrange("(p t) j -> t p j", t=TILES)
+    out_tiles = out.rearrange("b (p t) d -> (b t) p d", t=TILES)
 
     with ExitStack() as ctx:
         ctx.enter_context(tc.manual_schedule())
         keep = ctx.enter_context(tc.tile_pool(name="keep", bufs=1))
         x_pool = ctx.enter_context(tc.tile_pool(name="x", bufs=LOAD_AHEAD * ROUND_CHUNKS))
         adj_pool = ctx.enter_context(tc.tile_pool(name="adj", bufs=TILES))
-        grouped_pool = ctx.enter_context(tc.tile_pool(name="grouped", bufs=4))
-        code_pool = ctx.enter_context(tc.tile_pool(name="codes", bufs=6))
+        grouped_pool = ctx.enter_context(tc.tile_pool(name="grouped", bufs=6))
+        code_pool = ctx.enter_context(tc.tile_pool(name="codes", bufs=8))
         att_pool = ctx.enter_context(tc.tile_pool(name="attention", bufs=2))
         column_pool = ctx.enter_context(tc.tile_pool(name="columns", bufs=4))
         norm_pool = ctx.enter_context(tc.tile_pool(name="norm", bufs=3))
@@ -65,6 +67,10 @@ def tile_spatialprocessor_pa_k_kernel(
 
         w_planes = keep.tile([P, SKIP_PASSES, D], U8, align_bytes=64)
         nc.vector.memset(w_planes[:].bitcast(I32), 0)
+        gain_shift_rows = keep.tile([P, 2 * D], BF16)
+        nc.vector.memset(gain_shift_rows[:].bitcast(I32), 0)
+        ones = keep.tile([P, P], BF16)
+        nc.vector.memset(ones[:], 1.0)
         neg_half = keep.tile([P, 1], F32)
         nc.vector.memset(neg_half[:], -0.5)
         table_warm = keep.tile([P, 1], F32)
@@ -74,12 +80,12 @@ def tile_spatialprocessor_pa_k_kernel(
         ident_f32 = keep.tile([P, P], F32)
         masks.make_identity(nc, ident_f32[:])
 
+        nc.sync.dma_start(out=gain_shift_rows[0:1, 0:D], in_=ln_g.unsqueeze(0))
+        nc.sync.dma_start(out=gain_shift_rows[0:1, D : 2 * D], in_=ln_b.unsqueeze(0))
         q_rows = keep.tile([P, TILES, D], BF16)
         k_rows = keep.tile([P, TILES, D], BF16)
-        v_rows = keep.tile([P, TILES, D], BF16)
-        nc.sync.dma_start(out=q_rows[:], in_=q2.rearrange("b (t p) d -> p (b t) d", p=P))
-        nc.sync.dma_start(out=k_rows[:], in_=k2.rearrange("b (t p) d -> p (b t) d", p=P))
-        nc.sync.dma_start(out=v_rows[:], in_=v2.rearrange("b (t p) d -> p (b t) d", p=P))
+        nc.sync.dma_start(out=q_rows[:], in_=q2.rearrange("b (p t) d -> p (b t) d", t=TILES))
+        nc.sync.dma_start(out=k_rows[:], in_=k2.rearrange("b (p t) d -> p (b t) d", t=TILES))
 
         adj_tiles = []
         x_chunks = []
@@ -87,72 +93,89 @@ def tile_spatialprocessor_pa_k_kernel(
         def load_adj_tile():
             a = len(adj_tiles)
             adj_tile = adj_pool.tile([P, NODES], BF16, name="adj_tile")
-            nc.sync.dma_start(out=adj_tile[:], in_=adj[P * a : P * (a + 1), :])
+            nc.sync.dma_start(out=adj_tile[:], in_=adj_rows[a])
             adj_tiles.append(adj_tile)
 
         def load_round(n):
             for c in range(ROUND_CHUNKS * n, ROUND_CHUNKS * (n + 1)):
                 r, part = divmod(c, CHUNKS_PER_TILE)
                 x_chunk = x_pool.tile([P, CHUNK_K], BF16, name="x_chunk")
-                nc.sync.dma_start(
-                    out=x_chunk[:],
-                    in_=x_rows[P * r : P * (r + 1), CHUNK_K * part : CHUNK_K * (part + 1)],
-                )
+                nc.sync.dma_start(out=x_chunk[:], in_=x_tiles[r][:, CHUNK_K * part : CHUNK_K * (part + 1)])
                 x_chunks.append(x_chunk)
             if n % ROUNDS_PER_TILE == 0 and len(adj_tiles) < TILES:
                 load_adj_tile()
 
+        w_codes = keep.tile([P, SKIP_PASSES, D], U32, align_bytes=64)
+        w_words = proj_w_words.bitcast(I32).rearrange("g p n o -> p g (n o)")
+        w_scale_words = proj_w_scales.bitcast(I32)
+
+        def load_w_scales():
+            for quadrant in range(4):
+                nc.sync.dma_start(
+                    out=w_planes[32 * quadrant : 32 * quadrant + 4, :, :].bitcast(I32),
+                    in_=w_scale_words[:, 4 * quadrant : 4 * quadrant + 4, :].rearrange("g r n -> r g n"),
+                )
+
+        def load_w_codes(part):
+            passes = slice(CHUNK_PASSES * part, CHUNK_PASSES * (part + 1))
+            nc.sync.dma_start(out=w_codes[:, passes, :].bitcast(I32), in_=w_words[:, passes, :])
+
         load_adj_tile()
         load_round(0)
+        load_w_scales()
+        load_w_codes(0)
+        load_w_codes(1)
         load_round(1)
-        w_scale_words = proj_w_scales.bitcast(I32)
-        for quadrant in range(4):
-            nc.sync.dma_start(
-                out=w_planes[32 * quadrant : 32 * quadrant + 4, :, :].bitcast(I32),
-                in_=w_scale_words[:, 4 * quadrant : 4 * quadrant + 4, :].rearrange("g r n -> r g n"),
-            )
-        w_codes = keep.tile([P, SKIP_PASSES, D], U32, align_bytes=64)
-        nc.sync.dma_start(
-            out=w_codes[:].bitcast(I32),
-            in_=proj_w_words.bitcast(I32).rearrange("g p n o -> p g (n o)"),
-        )
-        gain = keep.tile([P, D], BF16)
-        shift = keep.tile([P, D], BF16)
-        nc.sync.dma_start(out=gain[:], in_=ln_g.partition_broadcast(P))
-        nc.sync.dma_start(out=shift[:], in_=ln_b.partition_broadcast(P))
+        load_w_codes(2)
+        load_w_codes(3)
+        v_rows = keep.tile([P, TILES, D], BF16)
+        nc.sync.dma_start(out=v_rows[:], in_=v2.rearrange("b (s p) d -> p (b s) d", p=P))
         for n in range(2, LOAD_AHEAD):
             load_round(n)
 
-        def flip_rows(rows, name):
-            bank = flip_psum.tile([P, TILES, P], BF16, name="qk_bank", tag="flip")
-            for t in range(TILES):
-                nc.tensor.transpose(bank[:, t, :], rows[:, t, :], ident_bf[:])
-            columns = keep.tile([P, NODES], BF16, name=name)
-            nc.scalar.copy(out=columns[:], in_=bank[:].rearrange("d t i -> d (t i)"))
-            return columns
+        gain_shift_bank = score_psum.tile([P, 2 * D], F32, name="gain_shift_bank", tag="score")
+        nc.tensor.matmul(out=gain_shift_bank[:], lhsT=ones[:], rhs=gain_shift_rows[:], start=True, stop=True)
+        gain_shift = keep.tile([P, 2 * D], F32)
+        nc.scalar.copy(out=gain_shift[:], in_=gain_shift_bank[:])
+        gain = gain_shift[:, 0:D]
+        shift = gain_shift[:, D : 2 * D]
 
-        q_cols = flip_rows(q_rows, "q_cols")
-        k_cols = flip_rows(k_rows, "k_cols")
-
-        v_grouped = keep.tile([P, KEY_PASSES, D, PACK], BF16, align_bytes=64)
-        for c in range(KEY_PASSES):
-            nc.vector.tensor_copy(
-                out=v_grouped[:, c],
-                in_=v_rows[:, PACK * c : PACK * (c + 1), :].rearrange("p t d -> p d t"),
-            )
-        v_codes = keep.tile([P, KEY_PASSES * D], U32, align_bytes=64)
-        v_planes = keep.tile([P, KEY_PASSES * D], U8, align_bytes=64)
-        nc.vector.quantize_mx(
-            out=v_codes[:].bitcast(FP8X4),
-            scales=v_planes[:],
-            in_=v_grouped[:].rearrange("p c d t -> p (c d t)"),
+        q_bank = flip_psum.tile([P, TILES, P], BF16, name="q_bank", tag="flip")
+        for t in range(TILES):
+            nc.tensor.transpose(q_bank[:, t, :], q_rows[:, t, :], ident_bf[:])
+        q_cols = keep.tile([P, TILES, P], BF16)
+        nc.scalar.copy(out=q_cols[:], in_=q_bank[:])
+        k_bank = flip_psum.tile([P, TILES, P], BF16, name="k_bank", tag="flip")
+        for t in range(TILES):
+            nc.tensor.transpose(k_bank[:, t, :], k_rows[:, t, :], ident_bf[:])
+        k_cols = keep.tile([P, NODES], BF16)
+        nc.scalar.copy(
+            out=k_cols[:].rearrange("d (p t) -> d p t", t=TILES), in_=k_bank[:].rearrange("d t p -> d p t")
         )
 
-        masked = {}
+        v_codes = keep.tile([P, KEY_PASSES * D], U32, align_bytes=64)
+        v_planes = keep.tile([P, KEY_PASSES * D], U8, align_bytes=64)
+
+        def quantise_v():
+            v_grouped = keep.tile([P, KEY_PASSES, D, PACK], BF16, align_bytes=64)
+            for c in range(KEY_PASSES):
+                nc.vector.tensor_copy(
+                    out=v_grouped[:, c],
+                    in_=v_rows[:, PACK * c : PACK * (c + 1), :].rearrange("p t d -> p d t"),
+                )
+            nc.vector.quantize_mx(
+                out=v_codes[:].bitcast(FP8X4),
+                scales=v_planes[:],
+                in_=v_grouped[:].rearrange("p c d t -> p (c d t)"),
+            )
+
+        neg_scores = {}
+        neg_max = {}
         e_rows = {}
         row_sums = {}
         e_grouped = {}
         e_operands = {}
+        h_banks = {}
         h_rows = {}
 
         def scores(m):
@@ -160,26 +183,28 @@ def tile_spatialprocessor_pa_k_kernel(
             if half == 0:
                 nc.vector.tensor_scalar(
                     out=adj_tiles[a][:], in0=adj_tiles[a][:],
-                    scalar1=0.0, scalar2=NEG_INF, op0=ALU.is_equal, op1=ALU.mult,
+                    scalar1=0.0, scalar2=PENALTY, op0=ALU.is_equal, op1=ALU.mult,
                 )
-                masked[a] = att_pool.tile([P, NODES], F32, name="masked")
+                neg_scores[a] = att_pool.tile([P, NODES], F32, name="neg_scores")
             keys = slice(BANK * half, BANK * (half + 1))
             bank = score_psum.tile([P, BANK], F32, name="score_bank", tag="score")
-            nc.tensor.matmul(
-                out=bank[:], lhsT=q_cols[:, P * a : P * (a + 1)], rhs=k_cols[:, keys], start=True, stop=True
-            )
-            nc.vector.scalar_tensor_tensor(
-                out=masked[a][:, keys], in0=bank[:], scalar=SCALE, in1=adj_tiles[a][:, keys],
-                op0=ALU.mult, op1=ALU.add,
+            nc.tensor.matmul(out=bank[:], lhsT=q_cols[:, a, :], rhs=k_cols[:, keys], start=True, stop=True)
+            nc.vector.tensor_tensor(
+                out=neg_scores[a][:, keys], in0=adj_tiles[a][:, keys], in1=bank[:], op=ALU.subtract
             )
 
-        def softmax(a):
-            neg_max = column_pool.tile([P, 1], F32, name="neg_max")
-            nc.vector.tensor_reduce(out=neg_max[:], in_=masked[a][:], axis=AXIS_X, op=ALU.max, negate=True)
+        def row_maximum(a):
+            neg_max[a] = column_pool.tile([P, 1], F32, name="neg_max")
+            nc.vector.tensor_scalar(
+                out=neg_scores[a][:], in0=neg_scores[a][:], scalar1=SCALE, scalar2=None,
+                op0=ALU.mult, op1=ALU.min, accum_out=neg_max[a][:],
+            )
+
+        def exponentials(a):
             e_rows[a] = att_pool.tile([P, NODES], BF16, name="e_rows")
             row_sums[a] = column_pool.tile([P, 1], F32, name="row_sum")
             nc.scalar.activation(
-                out=e_rows[a][:], in_=masked[a][:], func=ACT.Exp, bias=neg_max[:], scale=1.0,
+                out=e_rows[a][:], in_=neg_scores[a][:], func=ACT.Exp, bias=neg_max[a][:], scale=-1.0,
                 accum_out=row_sums[a][:],
             )
 
@@ -201,12 +226,12 @@ def tile_spatialprocessor_pa_k_kernel(
             nc.vector.reciprocal(out=inv_sum[:], in_=row_sums[a][:])
             e_operands[a] = (codes, planes, inv_sum)
 
-        def weighted_values(a):
+        def value_passes(a):
             codes, planes, inv_sum = e_operands[a]
-            bank = score_psum.tile([P, D], F32, name="h_bank", tag="score")
+            h_banks[a] = score_psum.tile([P, D], F32, name="h_bank", tag="score")
             for c in range(KEY_PASSES):
                 nc.tensor.matmul_mx(
-                    out=bank[:],
+                    out=h_banks[a][:],
                     lhsT=codes[:, P * c : P * (c + 1)].bitcast(FP8X4),
                     lhsT_scale=planes[:, P * c : P * (c + 1)],
                     rhs=v_codes[:, D * c : D * (c + 1)].bitcast(FP8X4),
@@ -214,9 +239,12 @@ def tile_spatialprocessor_pa_k_kernel(
                     start=(c == 0),
                     stop=(c == KEY_PASSES - 1),
                 )
+
+        def divide_by_row_sum(a):
+            inv_sum = e_operands[a][2]
             h_rows[a] = norm_pool.tile([P, D], F32, name="h_rows")
             nc.vector.tensor_scalar(
-                out=h_rows[a][:], in0=bank[:], scalar1=inv_sum[:], scalar2=None, op0=ALU.mult
+                out=h_rows[a][:], in0=h_banks[a][:], scalar1=inv_sum[:], scalar2=None, op0=ALU.mult
             )
 
         x_grouped = {}
@@ -278,53 +306,61 @@ def tile_spatialprocessor_pa_k_kernel(
             mean_var = column_pool.tile([P, 2], F32, name="mean_var")
             nc.vector.bn_aggr(out=mean_var[:], in_=stats[:])
             var_eps = column_pool.tile([P, 1], F32, name="var_eps")
-            nc.gpsimd.tensor_scalar(
+            nc.vector.tensor_scalar(
                 out=var_eps[:], in0=mean_var[:, 1:2], scalar1=LN_EPS, scalar2=None, op0=ALU.add
             )
             inv_std[r] = column_pool.tile([P, 1], F32, name="inv_std")
             nc.gpsimd.tensor_tensor(out=inv_std[r][:], in0=var_eps[:], in1=neg_half[:], op=ALU.pow)
             centred[r] = norm_pool.tile([P, D], F32, name="centred")
             nc.vector.scalar_tensor_tensor(
-                out=centred[r][:], in0=y[:], scalar=mean_var[:, 0:1], in1=gain[:],
+                out=centred[r][:], in0=y[:], scalar=mean_var[:, 0:1], in1=gain,
                 op0=ALU.subtract, op1=ALU.mult,
             )
 
         def norm_finish(r):
             result = norm_pool.tile([P, D], F32, name="result")
             nc.vector.scalar_tensor_tensor(
-                out=result[:], in0=centred[r][:], scalar=inv_std[r][:], in1=shift[:],
+                out=result[:], in0=centred[r][:], scalar=inv_std[r][:], in1=shift,
                 op0=ALU.mult, op1=ALU.add,
             )
-            nc.sync.dma_start(out=out_rows[P * r : P * (r + 1), :], in_=result[:])
+            nc.sync.dma_start(out=out_tiles[r], in_=result[:])
 
-        scores_issued = 0
-        for n in range(ROUNDS + 1):
-            first_of_tile = n % ROUNDS_PER_TILE == 0
-            closing = n // ROUNDS_PER_TILE - 1
-            if not first_of_tile and closing >= 0:
-                norm_finish(closing)
+        def is_tile(a):
+            return 0 <= a < TILES
+
+        for n in range(ROUNDS + 3):
+            a, second = divmod(n, ROUNDS_PER_TILE)
+            if 1 <= n <= ROUNDS:
+                quantise_x(ROUND_CHUNKS * n - 1)
+            if not second and is_tile(a - 2):
+                norm_finish(a - 2)
+            if n == ROUNDS_PER_TILE:
+                quantise_v()
+            if not second and is_tile(a - 1):
+                quantise_e(a - 1)
+            if second and is_tile(a - 1):
+                divide_by_row_sum(a - 1)
+                norm_statistics(a - 1)
             if n < ROUNDS:
                 flip_x(ROUND_CHUNKS * n)
-                scores_due = min(n + 2, TILES * SCORE_HALVES)
-                for m in range(scores_issued, scores_due):
-                    scores(m)
-                scores_issued = scores_due
+            if n == 0:
+                scores(0)
+                scores(1)
+            if not second and is_tile(a):
+                row_maximum(a)
+            if n + 2 < TILES * SCORE_HALVES:
+                scores(n + 2)
+            if n < ROUNDS:
+                quantise_x(ROUND_CHUNKS * n)
                 flip_x(ROUND_CHUNKS * n + 1)
                 if n + LOAD_AHEAD < ROUNDS:
                     load_round(n + LOAD_AHEAD)
-                if first_of_tile:
-                    softmax(n // ROUNDS_PER_TILE)
-                else:
-                    flip_e(n // ROUNDS_PER_TILE)
-                quantise_x(ROUND_CHUNKS * n)
-                quantise_x(ROUND_CHUNKS * n + 1)
-                if not first_of_tile:
-                    quantise_e(n // ROUNDS_PER_TILE)
-            if first_of_tile and closing >= 0:
-                weighted_values(closing)
-            if n >= 1:
+            if second and is_tile(a):
+                flip_e(a)
+            if not second and is_tile(a):
+                exponentials(a)
+            if not second and is_tile(a - 1):
+                value_passes(a - 1)
+            if 1 <= n <= ROUNDS:
                 skip_passes(ROUND_CHUNKS * (n - 1))
                 skip_passes(ROUND_CHUNKS * (n - 1) + 1)
-            if first_of_tile and closing >= 0:
-                norm_statistics(closing)
-        norm_finish(TILES - 1)

@@ -102,7 +102,7 @@ def tile_spatialprocessor_pa_k_kernel(
                 x_chunk = x_pool.tile([P, CHUNK_K], BF16, name="x_chunk")
                 nc.sync.dma_start(out=x_chunk[:], in_=x_tiles[r][:, CHUNK_K * part : CHUNK_K * (part + 1)])
                 x_chunks.append(x_chunk)
-            if n % ROUNDS_PER_TILE == 0 and len(adj_tiles) < TILES:
+            if (n == 0 or n % ROUNDS_PER_TILE == 1) and len(adj_tiles) < TILES:
                 load_adj_tile()
 
         w_codes = keep.tile([P, SKIP_PASSES, D], U32, align_bytes=64)
@@ -136,7 +136,7 @@ def tile_spatialprocessor_pa_k_kernel(
         gain_shift_bank = score_psum.tile([P, 2 * D], F32, name="gain_shift_bank", tag="score")
         nc.tensor.matmul(out=gain_shift_bank[:], lhsT=ones[:], rhs=gain_shift_rows[:], start=True, stop=True)
         gain_shift = keep.tile([P, 2 * D], F32)
-        nc.scalar.copy(out=gain_shift[:], in_=gain_shift_bank[:])
+        nc.vector.tensor_copy(out=gain_shift[:], in_=gain_shift_bank[:])
         gain = gain_shift[:, 0:D]
         shift = gain_shift[:, D : 2 * D]
 
@@ -144,7 +144,7 @@ def tile_spatialprocessor_pa_k_kernel(
         for t in range(TILES):
             nc.tensor.transpose(q_bank[:, t, :], q_rows[:, t, :], ident_bf[:])
         q_cols = keep.tile([P, TILES, P], BF16)
-        nc.scalar.copy(out=q_cols[:], in_=q_bank[:])
+        nc.vector.tensor_copy(out=q_cols[:], in_=q_bank[:])
         k_bank = flip_psum.tile([P, TILES, P], BF16, name="k_bank", tag="flip")
         for t in range(TILES):
             nc.tensor.transpose(k_bank[:, t, :], k_rows[:, t, :], ident_bf[:])
@@ -173,6 +173,7 @@ def tile_spatialprocessor_pa_k_kernel(
         neg_max = {}
         e_rows = {}
         row_sums = {}
+        e_banks = {}
         e_grouped = {}
         e_operands = {}
         h_banks = {}
@@ -209,11 +210,18 @@ def tile_spatialprocessor_pa_k_kernel(
             )
 
         def flip_e(a):
-            bank = flip_psum.tile([P, TILES, P], BF16, name="e_bank", tag="flip")
-            for s in range(TILES):
-                nc.tensor.transpose(bank[:, s, :], e_rows[a][:, P * s : P * (s + 1)], ident_bf[:])
             e_grouped[a] = att_pool.tile([P, KEY_PASSES, P, PACK], BF16, name="e_grouped", align_bytes=64)
-            nc.scalar.copy(out=e_grouped[a][:], in_=bank[:].rearrange("p (c t) i -> p c i t", t=PACK))
+            e_banks[a] = []
+            for c in range(KEY_PASSES):
+                bank = flip_psum.tile([P, PACK, P], BF16, name="e_bank", tag="flip")
+                for t in range(PACK):
+                    s = PACK * c + t
+                    nc.tensor.transpose(bank[:, t, :], e_rows[a][:, P * s : P * (s + 1)], ident_bf[:])
+                e_banks[a].append(bank)
+            nc.scalar.copy(out=e_grouped[a][:, 0], in_=e_banks[a][0][:].rearrange("p t i -> p i t"))
+
+        def regroup_e(a):
+            nc.vector.tensor_copy(out=e_grouped[a][:, 1], in_=e_banks[a][1][:].rearrange("p t i -> p i t"))
 
         def quantise_e(a):
             codes = att_pool.tile([P, KEY_PASSES * P], U32, name="e_codes", align_bytes=64)
@@ -325,42 +333,49 @@ def tile_spatialprocessor_pa_k_kernel(
             )
             nc.sync.dma_start(out=out_tiles[r], in_=result[:])
 
-        def is_tile(a):
-            return 0 <= a < TILES
+        def first_stage(a):
+            return max(2 * a - 1, 0)
+
+        def tiles_at_stage(n, stage):
+            return [a for a in range(TILES) if first_stage(a) + stage == n]
 
         for n in range(ROUNDS + 3):
-            a, second = divmod(n, ROUNDS_PER_TILE)
+            closed, second = divmod(n - 3, ROUNDS_PER_TILE)
+            for a in tiles_at_stage(n, 2):
+                regroup_e(a)
             if 1 <= n <= ROUNDS:
                 quantise_x(ROUND_CHUNKS * n - 1)
-            if not second and is_tile(a - 2):
-                norm_finish(a - 2)
+            if second and 0 <= closed < TILES:
+                norm_finish(closed)
             if n == ROUNDS_PER_TILE:
                 quantise_v()
-            if not second and is_tile(a - 1):
-                quantise_e(a - 1)
-            if second and is_tile(a - 1):
-                divide_by_row_sum(a - 1)
-                norm_statistics(a - 1)
+            for a in tiles_at_stage(n, 2):
+                quantise_e(a)
+            for a in tiles_at_stage(n, 3):
+                divide_by_row_sum(a)
+            if not second and 0 <= closed < TILES:
+                norm_statistics(closed)
             if n < ROUNDS:
                 flip_x(ROUND_CHUNKS * n)
             if n == 0:
                 scores(0)
                 scores(1)
-            if not second and is_tile(a):
+                scores(2)
+            for a in tiles_at_stage(n, 0):
                 row_maximum(a)
-            if n + 2 < TILES * SCORE_HALVES:
-                scores(n + 2)
+            if n + 3 < TILES * SCORE_HALVES:
+                scores(n + 3)
             if n < ROUNDS:
                 quantise_x(ROUND_CHUNKS * n)
                 flip_x(ROUND_CHUNKS * n + 1)
                 if n + LOAD_AHEAD < ROUNDS:
                     load_round(n + LOAD_AHEAD)
-            if second and is_tile(a):
+            for a in tiles_at_stage(n, 1):
                 flip_e(a)
-            if not second and is_tile(a):
+            for a in tiles_at_stage(n, 0):
                 exponentials(a)
-            if not second and is_tile(a - 1):
-                value_passes(a - 1)
+            for a in tiles_at_stage(n, 2):
+                value_passes(a)
             if 1 <= n <= ROUNDS:
                 skip_passes(ROUND_CHUNKS * (n - 1))
                 skip_passes(ROUND_CHUNKS * (n - 1) + 1)

@@ -25,6 +25,7 @@ KEY_PASSES = NODES // K_PASS
 SKIP_PASSES = F_IN // K_PASS
 BANK = 512
 SCORE_HALVES = NODES // BANK
+SCORE_PART = BANK // 2
 
 CHUNK_PASSES = 4
 CHUNK_K = CHUNK_PASSES * K_PASS
@@ -34,6 +35,7 @@ ROUND_CHUNKS = 2
 ROUNDS = CHUNKS // ROUND_CHUNKS
 ROUNDS_PER_TILE = ROUNDS // TILES
 LOAD_AHEAD = 12
+MX_LAG = 3
 
 SCALE = 1.0 / math.sqrt(D)
 NEG_INF = -1e9
@@ -169,6 +171,7 @@ def tile_spatialprocessor_pa_k_kernel(
                 in_=v_grouped[:].rearrange("p c d t -> p (c d t)"),
             )
 
+        score_banks = {}
         neg_scores = {}
         neg_max = {}
         e_rows = {}
@@ -179,20 +182,28 @@ def tile_spatialprocessor_pa_k_kernel(
         h_banks = {}
         h_rows = {}
 
-        def scores(m):
+        def score_matmul(m, part):
             a, half = divmod(m, SCORE_HALVES)
-            if half == 0:
-                nc.vector.tensor_scalar(
-                    out=adj_tiles[a][:], in0=adj_tiles[a][:],
-                    scalar1=0.0, scalar2=PENALTY, op0=ALU.is_equal, op1=ALU.mult,
-                )
-                neg_scores[a] = att_pool.tile([P, NODES], F32, name="neg_scores")
-            keys = slice(BANK * half, BANK * (half + 1))
-            bank = score_psum.tile([P, BANK], F32, name="score_bank", tag="score")
-            nc.tensor.matmul(out=bank[:], lhsT=q_cols[:, a, :], rhs=k_cols[:, keys], start=True, stop=True)
-            nc.vector.tensor_tensor(
-                out=neg_scores[a][:, keys], in0=adj_tiles[a][:, keys], in1=bank[:], op=ALU.subtract
+            if part == 0:
+                if half == 0:
+                    nc.vector.tensor_scalar(
+                        out=adj_tiles[a][:], in0=adj_tiles[a][:],
+                        scalar1=0.0, scalar2=PENALTY, op0=ALU.is_equal, op1=ALU.mult,
+                    )
+                    neg_scores[a] = att_pool.tile([P, NODES], F32, name="neg_scores")
+                score_banks[m] = score_psum.tile([P, BANK], F32, name="score_bank", tag="score")
+            bank = score_banks[m]
+            columns = slice(SCORE_PART * part, SCORE_PART * (part + 1))
+            first_key = BANK * half + SCORE_PART * part
+            nc.tensor.matmul(
+                out=bank[:, columns], lhsT=q_cols[:, a, :], rhs=k_cols[:, first_key : first_key + SCORE_PART],
+                start=True, stop=True,
             )
+            if part == 1:
+                keys = slice(BANK * half, BANK * (half + 1))
+                nc.vector.tensor_tensor(
+                    out=neg_scores[a][:, keys], in0=adj_tiles[a][:, keys], in1=bank[:], op=ALU.subtract
+                )
 
         def row_maximum(a):
             neg_max[a] = column_pool.tile([P, 1], F32, name="neg_max")
@@ -339,8 +350,14 @@ def tile_spatialprocessor_pa_k_kernel(
         def tiles_at_stage(n, stage):
             return [a for a in range(TILES) if first_stage(a) + stage == n]
 
-        for n in range(ROUNDS + 3):
-            closed, second = divmod(n - 3, ROUNDS_PER_TILE)
+        def multiply_chunk(c):
+            if 0 <= c < CHUNKS:
+                skip_passes(c)
+                if c % CHUNKS_PER_TILE == CHUNKS_PER_TILE - 1:
+                    value_passes(c // CHUNKS_PER_TILE)
+
+        for n in range(ROUNDS + 4):
+            closed, second = divmod(n - 4, ROUNDS_PER_TILE)
             for a in tiles_at_stage(n, 2):
                 regroup_e(a)
             if 1 <= n <= ROUNDS:
@@ -351,20 +368,23 @@ def tile_spatialprocessor_pa_k_kernel(
                 quantise_v()
             for a in tiles_at_stage(n, 2):
                 quantise_e(a)
-            for a in tiles_at_stage(n, 3):
-                divide_by_row_sum(a)
             if not second and 0 <= closed < TILES:
+                divide_by_row_sum(closed)
                 norm_statistics(closed)
+            if n > 0:
+                for a in tiles_at_stage(n, 0):
+                    row_maximum(a)
             if n < ROUNDS:
                 flip_x(ROUND_CHUNKS * n)
             if n == 0:
-                scores(0)
-                scores(1)
-                scores(2)
-            for a in tiles_at_stage(n, 0):
-                row_maximum(a)
+                for m in range(3):
+                    score_matmul(m, 0)
+                    score_matmul(m, 1)
+                    if m == 1:
+                        row_maximum(0)
             if n + 3 < TILES * SCORE_HALVES:
-                scores(n + 3)
+                score_matmul(n + 3, 0)
+            multiply_chunk(ROUND_CHUNKS * n - MX_LAG)
             if n < ROUNDS:
                 quantise_x(ROUND_CHUNKS * n)
                 flip_x(ROUND_CHUNKS * n + 1)
@@ -374,8 +394,6 @@ def tile_spatialprocessor_pa_k_kernel(
                 flip_e(a)
             for a in tiles_at_stage(n, 0):
                 exponentials(a)
-            for a in tiles_at_stage(n, 2):
-                value_passes(a)
-            if 1 <= n <= ROUNDS:
-                skip_passes(ROUND_CHUNKS * (n - 1))
-                skip_passes(ROUND_CHUNKS * (n - 1) + 1)
+            if n + 3 < TILES * SCORE_HALVES:
+                score_matmul(n + 3, 1)
+            multiply_chunk(ROUND_CHUNKS * n + 1 - MX_LAG)

@@ -34,8 +34,8 @@ CHUNKS = TILES * CHUNKS_PER_TILE
 ROUND_CHUNKS = 2
 ROUNDS = CHUNKS // ROUND_CHUNKS
 ROUNDS_PER_TILE = ROUNDS // TILES
+LAST_ATTENTION_ROUND = 11
 LOAD_AHEAD = 12
-MX_LAG = 3
 
 SCALE = 1.0 / math.sqrt(D)
 NEG_INF = -1e9
@@ -63,31 +63,26 @@ def tile_spatialprocessor_pa_k_kernel(
         att_pool = ctx.enter_context(tc.tile_pool(name="attention", bufs=2))
         column_pool = ctx.enter_context(tc.tile_pool(name="columns", bufs=4))
         norm_pool = ctx.enter_context(tc.tile_pool(name="norm", bufs=3))
+        result_pool = ctx.enter_context(tc.tile_pool(name="result", bufs=TILES))
         flip_psum = ctx.enter_context(tc.psum_pool(name="flip", bufs=4))
-        score_psum = ctx.enter_context(tc.psum_pool(name="score", bufs=2))
-        skip_psum = ctx.enter_context(tc.psum_pool(name="skip", bufs=2))
+        misc_psum = ctx.enter_context(tc.psum_pool(name="misc", bufs=2))
+        h_psum = ctx.enter_context(tc.psum_pool(name="h", bufs=1))
+        skip_psum = ctx.enter_context(tc.psum_pool(name="skip", bufs=1))
 
+        ident_f32 = keep.tile([P, P], F32)
+        masks.make_identity(nc, ident_f32[:])
+        ident_bf = keep.tile([P, P], BF16)
+        masks.make_identity(nc, ident_bf[:])
+        neg_half = keep.tile([P, 1], F32)
+        nc.vector.memset(neg_half[:], -0.5)
+        table_warm = keep.tile([P, 1], F32)
+        nc.scalar.activation(out=table_warm[:], in_=neg_half[:], func=ACT.Exp)
         w_planes = keep.tile([P, SKIP_PASSES, D], U8, align_bytes=64)
         nc.vector.memset(w_planes[:].bitcast(I32), 0)
         gain_shift_rows = keep.tile([P, 2 * D], BF16)
         nc.vector.memset(gain_shift_rows[:].bitcast(I32), 0)
         ones = keep.tile([P, P], BF16)
         nc.vector.memset(ones[:], 1.0)
-        neg_half = keep.tile([P, 1], F32)
-        nc.vector.memset(neg_half[:], -0.5)
-        table_warm = keep.tile([P, 1], F32)
-        nc.scalar.activation(out=table_warm[:], in_=neg_half[:], func=ACT.Exp)
-        ident_bf = keep.tile([P, P], BF16)
-        masks.make_identity(nc, ident_bf[:])
-        ident_f32 = keep.tile([P, P], F32)
-        masks.make_identity(nc, ident_f32[:])
-
-        nc.sync.dma_start(out=gain_shift_rows[0:1, 0:D], in_=ln_g.unsqueeze(0))
-        nc.sync.dma_start(out=gain_shift_rows[0:1, D : 2 * D], in_=ln_b.unsqueeze(0))
-        q_rows = keep.tile([P, TILES, D], BF16)
-        k_rows = keep.tile([P, TILES, D], BF16)
-        nc.sync.dma_start(out=q_rows[:], in_=q2.rearrange("b (p t) d -> p (b t) d", t=TILES))
-        nc.sync.dma_start(out=k_rows[:], in_=k2.rearrange("b (p t) d -> p (b t) d", t=TILES))
 
         adj_tiles = []
         x_chunks = []
@@ -98,13 +93,21 @@ def tile_spatialprocessor_pa_k_kernel(
             nc.sync.dma_start(out=adj_tile[:], in_=adj_rows[a])
             adj_tiles.append(adj_tile)
 
+        def load_chunk(pieces=1):
+            r, part = divmod(len(x_chunks), CHUNKS_PER_TILE)
+            x_chunk = x_pool.tile([P, CHUNK_K], BF16, name="x_chunk")
+            width = CHUNK_K // pieces
+            for i in range(pieces):
+                nc.sync.dma_start(
+                    out=x_chunk[:, width * i : width * (i + 1)],
+                    in_=x_tiles[r][:, CHUNK_K * part + width * i : CHUNK_K * part + width * (i + 1)],
+                )
+            x_chunks.append(x_chunk)
+
         def load_round(n):
-            for c in range(ROUND_CHUNKS * n, ROUND_CHUNKS * (n + 1)):
-                r, part = divmod(c, CHUNKS_PER_TILE)
-                x_chunk = x_pool.tile([P, CHUNK_K], BF16, name="x_chunk")
-                nc.sync.dma_start(out=x_chunk[:], in_=x_tiles[r][:, CHUNK_K * part : CHUNK_K * (part + 1)])
-                x_chunks.append(x_chunk)
-            if (n == 0 or n % ROUNDS_PER_TILE == 1) and len(adj_tiles) < TILES:
+            for _ in range(ROUND_CHUNKS):
+                load_chunk()
+            if n % ROUNDS_PER_TILE == 1 and len(adj_tiles) < TILES:
                 load_adj_tile()
 
         w_codes = keep.tile([P, SKIP_PASSES, D], U32, align_bytes=64)
@@ -122,49 +125,67 @@ def tile_spatialprocessor_pa_k_kernel(
             passes = slice(CHUNK_PASSES * part, CHUNK_PASSES * (part + 1))
             nc.sync.dma_start(out=w_codes[:, passes, :].bitcast(I32), in_=w_words[:, passes, :])
 
+        load_chunk(pieces=2)
+        q_rows = keep.tile([P, TILES, D], BF16)
+        k_rows = keep.tile([P, TILES, D], BF16)
+        nc.sync.dma_start(out=q_rows[:], in_=q2.rearrange("b (p t) d -> p (b t) d", t=TILES))
+        nc.sync.dma_start(out=k_rows[:], in_=k2.rearrange("b (p t) d -> p (b t) d", t=TILES))
+        load_chunk()
+        load_chunk()
         load_adj_tile()
-        load_round(0)
         load_w_scales()
+        load_chunk()
         load_w_codes(0)
         load_w_codes(1)
-        load_round(1)
+        load_adj_tile()
+        load_round(2)
         load_w_codes(2)
         load_w_codes(3)
-        v_rows = keep.tile([P, TILES, D], BF16)
-        nc.sync.dma_start(out=v_rows[:], in_=v2.rearrange("b (s p) d -> p (b s) d", p=P))
-        for n in range(2, LOAD_AHEAD):
+        nc.sync.dma_start(out=gain_shift_rows[0:1, 0:D], in_=ln_g.unsqueeze(0))
+        nc.sync.dma_start(out=gain_shift_rows[0:1, D : 2 * D], in_=ln_b.unsqueeze(0))
+        v_rows = keep.tile([P, KEY_PASSES, 2, 2, D], BF16)
+        nc.sync.dma_start(
+            out=v_rows[:].rearrange("p c u e d -> p (c u) (e d)"),
+            in_=v2.rearrange("b (s p e) d -> p (b s) (e d)", p=P, e=2),
+        )
+        for n in range(3, LOAD_AHEAD):
             load_round(n)
 
-        gain_shift_bank = score_psum.tile([P, 2 * D], F32, name="gain_shift_bank", tag="score")
-        nc.tensor.matmul(out=gain_shift_bank[:], lhsT=ones[:], rhs=gain_shift_rows[:], start=True, stop=True)
         gain_shift = keep.tile([P, 2 * D], F32)
-        nc.vector.tensor_copy(out=gain_shift[:], in_=gain_shift_bank[:])
         gain = gain_shift[:, 0:D]
         shift = gain_shift[:, D : 2 * D]
 
-        q_bank = flip_psum.tile([P, TILES, P], BF16, name="q_bank", tag="flip")
-        for t in range(TILES):
-            nc.tensor.transpose(q_bank[:, t, :], q_rows[:, t, :], ident_bf[:])
+        def spread_gain_shift():
+            bank = h_psum.tile([P, 2 * D], F32, name="gain_shift_bank", tag="h")
+            nc.tensor.matmul(out=bank[:], lhsT=ones[:], rhs=gain_shift_rows[:], start=True, stop=True)
+            nc.scalar.copy(out=gain_shift[:], in_=bank[:])
+
         q_cols = keep.tile([P, TILES, P], BF16)
-        nc.vector.tensor_copy(out=q_cols[:], in_=q_bank[:])
-        k_bank = flip_psum.tile([P, TILES, P], BF16, name="k_bank", tag="flip")
-        for t in range(TILES):
-            nc.tensor.transpose(k_bank[:, t, :], k_rows[:, t, :], ident_bf[:])
         k_cols = keep.tile([P, NODES], BF16)
-        nc.scalar.copy(
-            out=k_cols[:].rearrange("d (p t) -> d p t", t=TILES), in_=k_bank[:].rearrange("d t p -> d p t")
-        )
+
+        def flip_q_and_k():
+            q_bank = misc_psum.tile([P, TILES, P], BF16, name="q_bank", tag="misc")
+            for t in range(TILES):
+                nc.tensor.transpose(q_bank[:, t, :], q_rows[:, t, :], ident_bf[:])
+            nc.vector.tensor_copy(out=q_cols[:], in_=q_bank[:])
+            k_bank = misc_psum.tile([P, TILES, P], BF16, name="k_bank", tag="misc")
+            for t in range(TILES):
+                nc.tensor.transpose(k_bank[:, t, :], k_rows[:, t, :], ident_bf[:])
+            nc.vector.tensor_copy(
+                out=k_cols[:].rearrange("d (p t) -> d p t", t=TILES), in_=k_bank[:].rearrange("d t p -> d p t")
+            )
 
         v_codes = keep.tile([P, KEY_PASSES * D], U32, align_bytes=64)
         v_planes = keep.tile([P, KEY_PASSES * D], U8, align_bytes=64)
+        v_grouped = keep.tile([P, KEY_PASSES, D, PACK], BF16, align_bytes=64)
 
-        def quantise_v():
-            v_grouped = keep.tile([P, KEY_PASSES, D, PACK], BF16, align_bytes=64)
+        def regroup_v():
             for c in range(KEY_PASSES):
                 nc.vector.tensor_copy(
-                    out=v_grouped[:, c],
-                    in_=v_rows[:, PACK * c : PACK * (c + 1), :].rearrange("p t d -> p d t"),
+                    out=v_grouped[:, c], in_=v_rows[:, c].rearrange("p u e d -> p d (u e)")
                 )
+
+        def quantise_v():
             nc.vector.quantize_mx(
                 out=v_codes[:].bitcast(FP8X4),
                 scales=v_planes[:],
@@ -180,30 +201,26 @@ def tile_spatialprocessor_pa_k_kernel(
         e_grouped = {}
         e_operands = {}
         h_banks = {}
-        h_rows = {}
 
-        def score_matmul(m, part):
-            a, half = divmod(m, SCORE_HALVES)
-            if part == 0:
-                if half == 0:
-                    nc.vector.tensor_scalar(
-                        out=adj_tiles[a][:], in0=adj_tiles[a][:],
-                        scalar1=0.0, scalar2=PENALTY, op0=ALU.is_equal, op1=ALU.mult,
-                    )
-                    neg_scores[a] = att_pool.tile([P, NODES], F32, name="neg_scores")
-                score_banks[m] = score_psum.tile([P, BANK], F32, name="score_bank", tag="score")
-            bank = score_banks[m]
-            columns = slice(SCORE_PART * part, SCORE_PART * (part + 1))
-            first_key = BANK * half + SCORE_PART * part
-            nc.tensor.matmul(
-                out=bank[:, columns], lhsT=q_cols[:, a, :], rhs=k_cols[:, first_key : first_key + SCORE_PART],
-                start=True, stop=True,
+        def penalties(a):
+            nc.vector.tensor_scalar(
+                out=adj_tiles[a][:], in0=adj_tiles[a][:],
+                scalar1=0.0, scalar2=PENALTY, op0=ALU.is_equal, op1=ALU.mult,
             )
-            if part == 1:
-                keys = slice(BANK * half, BANK * (half + 1))
-                nc.vector.tensor_tensor(
-                    out=neg_scores[a][:, keys], in0=adj_tiles[a][:, keys], in1=bank[:], op=ALU.subtract
-                )
+
+        def score_matmul(a, half):
+            bank = misc_psum.tile([P, BANK], F32, name="score_bank", tag="misc")
+            keys = slice(BANK * half, BANK * (half + 1))
+            nc.tensor.matmul(out=bank[:], lhsT=q_cols[:, a, :], rhs=k_cols[:, keys], start=True, stop=True)
+            score_banks[a, half] = bank
+
+        def mask_scores(a, half):
+            if half == 0:
+                neg_scores[a] = att_pool.tile([P, NODES], F32, name="neg_scores")
+            keys = slice(BANK * half, BANK * (half + 1))
+            nc.vector.tensor_tensor(
+                out=neg_scores[a][:, keys], in0=adj_tiles[a][:, keys], in1=score_banks[a, half][:], op=ALU.subtract
+            )
 
         def row_maximum(a):
             neg_max[a] = column_pool.tile([P, 1], F32, name="neg_max")
@@ -221,18 +238,19 @@ def tile_spatialprocessor_pa_k_kernel(
             )
 
         def flip_e(a):
-            e_grouped[a] = att_pool.tile([P, KEY_PASSES, P, PACK], BF16, name="e_grouped", align_bytes=64)
-            e_banks[a] = []
+            words = e_rows[a][:].bitcast(F32)
+            bank = flip_psum.tile([P, KEY_PASSES, 2, P], F32, name="e_bank", tag="flip")
             for c in range(KEY_PASSES):
-                bank = flip_psum.tile([P, PACK, P], BF16, name="e_bank", tag="flip")
-                for t in range(PACK):
-                    s = PACK * c + t
-                    nc.tensor.transpose(bank[:, t, :], e_rows[a][:, P * s : P * (s + 1)], ident_bf[:])
-                e_banks[a].append(bank)
-            nc.scalar.copy(out=e_grouped[a][:, 0], in_=e_banks[a][0][:].rearrange("p t i -> p i t"))
+                for u in range(2):
+                    first = P * (2 * c + u)
+                    nc.tensor.transpose(bank[:, c, u, :], words[:, first : first + P], ident_f32[:])
+            e_banks[a] = bank
 
         def regroup_e(a):
-            nc.vector.tensor_copy(out=e_grouped[a][:, 1], in_=e_banks[a][1][:].rearrange("p t i -> p i t"))
+            e_grouped[a] = att_pool.tile([P, KEY_PASSES, P, PACK], BF16, name="e_grouped", align_bytes=64)
+            nc.scalar.copy(
+                out=e_grouped[a][:].bitcast(F32), in_=e_banks[a][:].rearrange("p c u i -> p c i u")
+            )
 
         def quantise_e(a):
             codes = att_pool.tile([P, KEY_PASSES * P], U32, name="e_codes", align_bytes=64)
@@ -246,8 +264,8 @@ def tile_spatialprocessor_pa_k_kernel(
             e_operands[a] = (codes, planes, inv_sum)
 
         def value_passes(a):
-            codes, planes, inv_sum = e_operands[a]
-            h_banks[a] = score_psum.tile([P, D], F32, name="h_bank", tag="score")
+            codes, planes = e_operands[a][0:2]
+            h_banks[a] = h_psum.tile([P, D], F32, name="h_bank", tag="h")
             for c in range(KEY_PASSES):
                 nc.tensor.matmul_mx(
                     out=h_banks[a][:],
@@ -259,18 +277,12 @@ def tile_spatialprocessor_pa_k_kernel(
                     stop=(c == KEY_PASSES - 1),
                 )
 
-        def divide_by_row_sum(a):
-            inv_sum = e_operands[a][2]
-            h_rows[a] = norm_pool.tile([P, D], F32, name="h_rows")
-            nc.vector.tensor_scalar(
-                out=h_rows[a][:], in0=h_banks[a][:], scalar1=inv_sum[:], scalar2=None, op0=ALU.mult
-            )
-
         x_grouped = {}
         x_operands = {}
         skip_banks = {}
+        skip_rows = {}
 
-        def flip_x(c):
+        def flip_x(c, vector_copies=()):
             words = x_chunks[c][:].bitcast(F32)
             x_grouped[c] = grouped_pool.tile([P, CHUNK_PASSES, P, PACK], BF16, name="x_grouped", align_bytes=64)
             grouped_words = x_grouped[c][:].bitcast(F32)
@@ -284,17 +296,19 @@ def tile_spatialprocessor_pa_k_kernel(
                             words[:, start_word + u : start_word + K_PASS // 2 : 2],
                             ident_f32[:],
                         )
-                nc.scalar.copy(
-                    out=grouped_words[:, first : first + 2], in_=bank[:].rearrange("p g u n -> p g n u")
-                )
+                copy = nc.vector.tensor_copy if first in vector_copies else nc.scalar.copy
+                copy(out=grouped_words[:, first : first + 2], in_=bank[:].rearrange("p g u n -> p g n u"))
 
-        def quantise_x(c):
+        def quantise_x(c, pieces=1):
             codes = code_pool.tile([P, CHUNK_PASSES * P], U32, name="x_codes", align_bytes=64)
             planes = code_pool.tile([P, CHUNK_PASSES * P], U8, name="x_planes", align_bytes=64)
-            nc.vector.quantize_mx(
-                out=codes[:].bitcast(FP8X4), scales=planes[:],
-                in_=x_grouped[c][:].rearrange("p g n t -> p (g n t)"),
-            )
+            passes = CHUNK_PASSES // pieces
+            for i in range(pieces):
+                columns = slice(P * passes * i, P * passes * (i + 1))
+                nc.vector.quantize_mx(
+                    out=codes[:, columns].bitcast(FP8X4), scales=planes[:, columns],
+                    in_=x_grouped[c][:, passes * i : passes * (i + 1)].rearrange("p g n t -> p (g n t)"),
+                )
             x_operands[c] = (codes, planes)
 
         def skip_passes(c):
@@ -314,86 +328,126 @@ def tile_spatialprocessor_pa_k_kernel(
                     stop=(w_pass == SKIP_PASSES - 1),
                 )
 
+        y_rows = {}
+        stats = {}
+        mean_var = {}
         centred = {}
         inv_std = {}
 
-        def norm_statistics(r):
-            y = norm_pool.tile([P, D], F32, name="y")
-            nc.vector.tensor_tensor(out=y[:], in0=skip_banks[r][:], in1=h_rows[r][:], op=ALU.add)
-            stats = column_pool.tile([P, 6], F32, name="stats")
-            nc.vector.bn_stats(out=stats[:], in_=y[:])
-            mean_var = column_pool.tile([P, 2], F32, name="mean_var")
-            nc.vector.bn_aggr(out=mean_var[:], in_=stats[:])
+        h_rows = {}
+
+        def divide_by_row_sum(a):
+            h_rows[a] = norm_pool.tile([P, D], F32, name="h_rows")
+            nc.scalar.activation(out=h_rows[a][:], in_=h_banks[a][:], func=ACT.Copy, scale=e_operands[a][2][:])
+
+        def take_skip(r):
+            skip_rows[r] = norm_pool.tile([P, D], F32, name="skip_rows")
+            nc.scalar.copy(out=skip_rows[r][:], in_=skip_banks[r][:])
+
+        def add_streams(r):
+            y_rows[r] = norm_pool.tile([P, D], F32, name="y")
+            if r == TILES - 1:
+                nc.vector.tensor_tensor(out=y_rows[r][:], in0=skip_banks[r][:], in1=h_rows[r][:], op=ALU.add)
+                return
+            nc.vector.scalar_tensor_tensor(
+                out=y_rows[r][:], in0=h_banks[r][:], scalar=e_operands[r][2][:], in1=skip_rows[r][:],
+                op0=ALU.mult, op1=ALU.add,
+            )
+
+        def norm_stats(r):
+            stats[r] = column_pool.tile([P, 6], F32, name="stats")
+            nc.vector.bn_stats(out=stats[r][:], in_=y_rows[r][:])
+
+        def norm_moments(r):
+            mean_var[r] = column_pool.tile([P, 2], F32, name="mean_var")
+            nc.vector.bn_aggr(out=mean_var[r][:], in_=stats[r][:])
             var_eps = column_pool.tile([P, 1], F32, name="var_eps")
-            nc.vector.tensor_scalar(
-                out=var_eps[:], in0=mean_var[:, 1:2], scalar1=LN_EPS, scalar2=None, op0=ALU.add
+            nc.gpsimd.tensor_scalar(
+                out=var_eps[:], in0=mean_var[r][:, 1:2], scalar1=LN_EPS, scalar2=None, op0=ALU.add
             )
             inv_std[r] = column_pool.tile([P, 1], F32, name="inv_std")
             nc.gpsimd.tensor_tensor(out=inv_std[r][:], in0=var_eps[:], in1=neg_half[:], op=ALU.pow)
+
+        def norm_centre(r):
             centred[r] = norm_pool.tile([P, D], F32, name="centred")
             nc.vector.scalar_tensor_tensor(
-                out=centred[r][:], in0=y[:], scalar=mean_var[:, 0:1], in1=gain,
+                out=centred[r][:], in0=y_rows[r][:], scalar=mean_var[r][:, 0:1], in1=gain,
                 op0=ALU.subtract, op1=ALU.mult,
             )
 
         def norm_finish(r):
-            result = norm_pool.tile([P, D], F32, name="result")
+            result = result_pool.tile([P, D], F32, name="result")
             nc.vector.scalar_tensor_tensor(
                 out=result[:], in0=centred[r][:], scalar=inv_std[r][:], in1=shift,
                 op0=ALU.mult, op1=ALU.add,
             )
             nc.sync.dma_start(out=out_tiles[r], in_=result[:])
 
-        def first_stage(a):
-            return max(2 * a - 1, 0)
+        def first_round(a):
+            return a * LAST_ATTENTION_ROUND // (TILES - 1)
 
-        def tiles_at_stage(n, stage):
-            return [a for a in range(TILES) if first_stage(a) + stage == n]
+        def at(n, stage):
+            return [a for a in range(TILES) if first_round(a) + stage == n]
 
-        def multiply_chunk(c):
-            if 0 <= c < CHUNKS:
-                skip_passes(c)
-                if c % CHUNKS_PER_TILE == CHUNKS_PER_TILE - 1:
-                    value_passes(c // CHUNKS_PER_TILE)
+        def norm_tile(n):
+            tiles = [r for r in range(TILES) if max(2 * r + 3, first_round(r) + 5) == n]
+            return tiles[0] if tiles else None
 
-        for n in range(ROUNDS + 4):
-            closed, second = divmod(n - 4, ROUNDS_PER_TILE)
-            for a in tiles_at_stage(n, 2):
-                regroup_e(a)
+        for n in range(ROUNDS + 3):
+            closing = norm_tile(n)
+            finishing = norm_tile(n - 1)
+            taken, odd = divmod(n - 3, 2)
+            if not odd and 0 <= taken < TILES - 1:
+                take_skip(taken)
             if 1 <= n <= ROUNDS:
-                quantise_x(ROUND_CHUNKS * n - 1)
-            if second and 0 <= closed < TILES:
-                norm_finish(closed)
-            if n == ROUNDS_PER_TILE:
+                quantise_x(2 * n - 1, 2 if n == ROUNDS else 1)
+            if n == 3:
                 quantise_v()
-            for a in tiles_at_stage(n, 2):
+            if finishing is not None:
+                norm_finish(finishing)
+            for a in at(n, 4):
                 quantise_e(a)
-            if not second and 0 <= closed < TILES:
-                divide_by_row_sum(closed)
-                norm_statistics(closed)
-            if n > 0:
-                for a in tiles_at_stage(n, 0):
-                    row_maximum(a)
+            if closing is not None:
+                add_streams(closing)
+            for a in at(n, 1):
+                mask_scores(a, 0)
+            if closing is not None:
+                norm_stats(closing)
+            for a in at(n, 1):
+                mask_scores(a, 1)
+            if closing is not None:
+                norm_moments(closing)
+            for a in at(n, 2):
+                row_maximum(a)
+            if closing is not None:
+                norm_centre(closing)
             if n < ROUNDS:
-                flip_x(ROUND_CHUNKS * n)
-            if n == 0:
-                for m in range(3):
-                    score_matmul(m, 0)
-                    score_matmul(m, 1)
-                    if m == 1:
-                        row_maximum(0)
-            if n + 3 < TILES * SCORE_HALVES:
-                score_matmul(n + 3, 0)
-            multiply_chunk(ROUND_CHUNKS * n - MX_LAG)
+                flip_x(2 * n)
+                if n == 0:
+                    flip_q_and_k()
+                flip_x(2 * n + 1, (2,) if n == ROUNDS - 1 else ())
+            for a in at(n, 0):
+                penalties(a)
+            if n == 2:
+                regroup_v()
             if n < ROUNDS:
-                quantise_x(ROUND_CHUNKS * n)
-                flip_x(ROUND_CHUNKS * n + 1)
+                quantise_x(2 * n)
                 if n + LOAD_AHEAD < ROUNDS:
                     load_round(n + LOAD_AHEAD)
-            for a in tiles_at_stage(n, 1):
+            for a in at(n, 3):
                 flip_e(a)
-            for a in tiles_at_stage(n, 0):
+                regroup_e(a)
+            for a in at(n, 0):
+                score_matmul(a, 0)
+                score_matmul(a, 1)
+            if n == 3:
+                spread_gain_shift()
+            for a in at(n, 2):
                 exponentials(a)
-            if n + 3 < TILES * SCORE_HALVES:
-                score_matmul(n + 3, 1)
-            multiply_chunk(ROUND_CHUNKS * n + 1 - MX_LAG)
+            for a in at(n, 4):
+                value_passes(a)
+                if a == TILES - 1:
+                    divide_by_row_sum(a)
+            if 1 <= n <= ROUNDS:
+                skip_passes(2 * n - 2)
+                skip_passes(2 * n - 1)

@@ -34,12 +34,11 @@ CHUNKS = TILES * CHUNKS_PER_TILE
 ROUND_CHUNKS = 2
 ROUNDS = CHUNKS // ROUND_CHUNKS
 ROUNDS_PER_TILE = ROUNDS // TILES
-LAST_ATTENTION_ROUND = 11
+LAST_ATTENTION_ROUND = 10
 LOAD_AHEAD = 12
 
 SCALE = 1.0 / math.sqrt(D)
-NEG_INF = -1e9
-PENALTY = -NEG_INF / SCALE
+PENALTY = 2.0**34
 LN_EPS = 1e-3
 
 FLOPS = 2 * NODES * NODES * D * 2 + 2 * NODES * F_IN * D
@@ -60,7 +59,7 @@ def tile_spatialprocessor_pa_k_kernel(
         adj_pool = ctx.enter_context(tc.tile_pool(name="adj", bufs=TILES))
         grouped_pool = ctx.enter_context(tc.tile_pool(name="grouped", bufs=6))
         code_pool = ctx.enter_context(tc.tile_pool(name="codes", bufs=8))
-        att_pool = ctx.enter_context(tc.tile_pool(name="attention", bufs=2))
+        att_pool = ctx.enter_context(tc.tile_pool(name="attention", bufs=3))
         column_pool = ctx.enter_context(tc.tile_pool(name="columns", bufs=4))
         norm_pool = ctx.enter_context(tc.tile_pool(name="norm", bufs=3))
         result_pool = ctx.enter_context(tc.tile_pool(name="result", bufs=TILES))
@@ -84,6 +83,24 @@ def tile_spatialprocessor_pa_k_kernel(
         ones = keep.tile([P, P], BF16)
         nc.vector.memset(ones[:], 1.0)
 
+        def first_slot(a):
+            return 2 * (a * LAST_ATTENTION_ROUND // (TILES - 1)) + 1
+
+        def at(c, stage):
+            return [a for a in range(TILES) if first_slot(a) + stage == c]
+
+        def value_slot(a):
+            return first_slot(a) + 10
+
+        def skip_taken(r):
+            return CHUNKS_PER_TILE * r + 6
+
+        def h_comes_first(r):
+            return value_slot(r) + 2 <= skip_taken(r)
+
+        def norm_tiles(c):
+            return [r for r in range(TILES) if max(skip_taken(r), value_slot(r) + 1) == c]
+
         adj_tiles = []
         x_chunks = []
 
@@ -105,10 +122,10 @@ def tile_spatialprocessor_pa_k_kernel(
             x_chunks.append(x_chunk)
 
         def load_round(n):
+            for _ in at(2 * n, 1):
+                load_adj_tile()
             for _ in range(ROUND_CHUNKS):
                 load_chunk()
-            if n % ROUNDS_PER_TILE == 1 and len(adj_tiles) < TILES:
-                load_adj_tile()
 
         w_codes = keep.tile([P, SKIP_PASSES, D], U32, align_bytes=64)
         w_words = proj_w_words.bitcast(I32).rearrange("g p n o -> p g (n o)")
@@ -125,30 +142,39 @@ def tile_spatialprocessor_pa_k_kernel(
             passes = slice(CHUNK_PASSES * part, CHUNK_PASSES * (part + 1))
             nc.sync.dma_start(out=w_codes[:, passes, :].bitcast(I32), in_=w_words[:, passes, :])
 
-        load_chunk(pieces=2)
         q_rows = keep.tile([P, TILES, D], BF16)
         k_rows = keep.tile([P, TILES, D], BF16)
-        nc.sync.dma_start(out=q_rows[:], in_=q2.rearrange("b (p t) d -> p (b t) d", t=TILES))
-        nc.sync.dma_start(out=k_rows[:], in_=k2.rearrange("b (p t) d -> p (b t) d", t=TILES))
+        v_rows = keep.tile([P, KEY_PASSES, 2, 2, D], BF16)
+
+        def load_q_and_k():
+            nc.sync.dma_start(out=q_rows[:], in_=q2.rearrange("b (p t) d -> p (b t) d", t=TILES))
+            nc.sync.dma_start(out=k_rows[:], in_=k2.rearrange("b (p t) d -> p (b t) d", t=TILES))
+
+        def load_v():
+            nc.sync.dma_start(
+                out=v_rows[:].rearrange("p c u e d -> p (c u) (e d)"),
+                in_=v2.rearrange("b (s p e) d -> p (b s) (e d)", p=P, e=2),
+            )
+
+        def load_gain_shift():
+            nc.sync.dma_start(out=gain_shift_rows[0:1, 0:D], in_=ln_g.unsqueeze(0))
+            nc.sync.dma_start(out=gain_shift_rows[0:1, D : 2 * D], in_=ln_b.unsqueeze(0))
+
+        load_chunk(pieces=2)
+        load_q_and_k()
         load_chunk()
-        load_chunk()
-        load_adj_tile()
+        load_round(1)
         load_w_scales()
-        load_chunk()
         load_w_codes(0)
         load_w_codes(1)
-        load_adj_tile()
         load_round(2)
         load_w_codes(2)
         load_w_codes(3)
-        nc.sync.dma_start(out=gain_shift_rows[0:1, 0:D], in_=ln_g.unsqueeze(0))
-        nc.sync.dma_start(out=gain_shift_rows[0:1, D : 2 * D], in_=ln_b.unsqueeze(0))
-        v_rows = keep.tile([P, KEY_PASSES, 2, 2, D], BF16)
-        nc.sync.dma_start(
-            out=v_rows[:].rearrange("p c u e d -> p (c u) (e d)"),
-            in_=v2.rearrange("b (s p e) d -> p (b s) (e d)", p=P, e=2),
-        )
-        for n in range(3, LOAD_AHEAD):
+        load_round(3)
+        load_round(4)
+        load_v()
+        load_gain_shift()
+        for n in range(5, LOAD_AHEAD):
             load_round(n)
 
         gain_shift = keep.tile([P, 2 * D], F32)
@@ -167,7 +193,9 @@ def tile_spatialprocessor_pa_k_kernel(
             q_bank = misc_psum.tile([P, TILES, P], BF16, name="q_bank", tag="misc")
             for t in range(TILES):
                 nc.tensor.transpose(q_bank[:, t, :], q_rows[:, t, :], ident_bf[:])
-            nc.vector.tensor_copy(out=q_cols[:], in_=q_bank[:])
+            nc.vector.tensor_scalar(
+                out=q_cols[:], in0=q_bank[:], scalar1=1.0 / PENALTY, scalar2=None, op0=ALU.mult
+            )
             k_bank = misc_psum.tile([P, TILES, P], BF16, name="k_bank", tag="misc")
             for t in range(TILES):
                 nc.tensor.transpose(k_bank[:, t, :], k_rows[:, t, :], ident_bf[:])
@@ -202,12 +230,6 @@ def tile_spatialprocessor_pa_k_kernel(
         e_operands = {}
         h_banks = {}
 
-        def penalties(a):
-            nc.vector.tensor_scalar(
-                out=adj_tiles[a][:], in0=adj_tiles[a][:],
-                scalar1=0.0, scalar2=PENALTY, op0=ALU.is_equal, op1=ALU.mult,
-            )
-
         def score_matmul(a, half):
             bank = misc_psum.tile([P, BANK], F32, name="score_bank", tag="misc")
             keys = slice(BANK * half, BANK * (half + 1))
@@ -218,14 +240,15 @@ def tile_spatialprocessor_pa_k_kernel(
             if half == 0:
                 neg_scores[a] = att_pool.tile([P, NODES], F32, name="neg_scores")
             keys = slice(BANK * half, BANK * (half + 1))
-            nc.vector.tensor_tensor(
-                out=neg_scores[a][:, keys], in0=adj_tiles[a][:, keys], in1=score_banks[a, half][:], op=ALU.subtract
+            nc.vector.scalar_tensor_tensor(
+                out=neg_scores[a][:, keys], in0=adj_tiles[a][:, keys], scalar=0.0, in1=score_banks[a, half][:],
+                op0=ALU.is_equal, op1=ALU.subtract,
             )
 
         def row_maximum(a):
             neg_max[a] = column_pool.tile([P, 1], F32, name="neg_max")
             nc.vector.tensor_scalar(
-                out=neg_scores[a][:], in0=neg_scores[a][:], scalar1=SCALE, scalar2=None,
+                out=neg_scores[a][:], in0=neg_scores[a][:], scalar1=PENALTY * SCALE, scalar2=None,
                 op0=ALU.mult, op1=ALU.min, accum_out=neg_max[a][:],
             )
 
@@ -346,7 +369,7 @@ def tile_spatialprocessor_pa_k_kernel(
 
         def add_streams(r):
             y_rows[r] = norm_pool.tile([P, D], F32, name="y")
-            if r == TILES - 1:
+            if h_comes_first(r):
                 nc.vector.tensor_tensor(out=y_rows[r][:], in0=skip_banks[r][:], in1=h_rows[r][:], op=ALU.add)
                 return
             nc.vector.scalar_tensor_tensor(
@@ -383,71 +406,66 @@ def tile_spatialprocessor_pa_k_kernel(
             )
             nc.sync.dma_start(out=out_tiles[r], in_=result[:])
 
-        def first_round(a):
-            return a * LAST_ATTENTION_ROUND // (TILES - 1)
+        def multiply(chunks):
+            for c in chunks:
+                if 0 <= c < CHUNKS:
+                    skip_passes(c)
 
-        def at(n, stage):
-            return [a for a in range(TILES) if first_round(a) + stage == n]
-
-        def norm_tile(n):
-            tiles = [r for r in range(TILES) if max(2 * r + 3, first_round(r) + 5) == n]
-            return tiles[0] if tiles else None
-
-        for n in range(ROUNDS + 3):
-            closing = norm_tile(n)
-            finishing = norm_tile(n - 1)
-            taken, odd = divmod(n - 3, 2)
-            if not odd and 0 <= taken < TILES - 1:
-                take_skip(taken)
-            if 1 <= n <= ROUNDS:
-                quantise_x(2 * n - 1, 2 if n == ROUNDS else 1)
-            if n == 3:
+        for c in range(CHUNKS + 1):
+            last = c == CHUNKS
+            opening_ln, closing_ln, finishing_ln = norm_tiles(c), norm_tiles(c - 1), norm_tiles(c - 2)
+            for r in range(TILES):
+                if c == skip_taken(r) and not h_comes_first(r):
+                    take_skip(r)
+            if c >= 1:
+                quantise_x(c - 1, 2 if last else 1)
+            if c == 11:
                 quantise_v()
-            if finishing is not None:
-                norm_finish(finishing)
-            for a in at(n, 4):
-                quantise_e(a)
-            if closing is not None:
-                add_streams(closing)
-            for a in at(n, 1):
+            for r in opening_ln:
+                if r < TILES - 1:
+                    add_streams(r)
+            for r in closing_ln:
+                norm_moments(r)
+            for a in at(c, 1):
                 mask_scores(a, 0)
-            if closing is not None:
-                norm_stats(closing)
-            for a in at(n, 1):
                 mask_scores(a, 1)
-            if closing is not None:
-                norm_moments(closing)
-            for a in at(n, 2):
+            for a in at(c, 3):
                 row_maximum(a)
-            if closing is not None:
-                norm_centre(closing)
-            if n < ROUNDS:
-                flip_x(2 * n)
-                if n == 0:
-                    flip_q_and_k()
-                flip_x(2 * n + 1, (2,) if n == ROUNDS - 1 else ())
-            for a in at(n, 0):
-                penalties(a)
-            if n == 2:
-                regroup_v()
-            if n < ROUNDS:
-                quantise_x(2 * n)
-                if n + LOAD_AHEAD < ROUNDS:
-                    load_round(n + LOAD_AHEAD)
-            for a in at(n, 3):
+            for a in at(c, 8):
+                quantise_e(a)
+            for r in finishing_ln:
+                norm_finish(r)
+            if not last:
+                flip_x(c, ())
+            if c == 0:
+                flip_q_and_k()
+            for a in at(c, 6):
                 flip_e(a)
                 regroup_e(a)
-            for a in at(n, 0):
-                score_matmul(a, 0)
-                score_matmul(a, 1)
-            if n == 3:
-                spread_gain_shift()
-            for a in at(n, 2):
+            for a in at(c, 4):
                 exponentials(a)
-            for a in at(n, 4):
-                value_passes(a)
-                if a == TILES - 1:
+            for a in range(TILES):
+                if c == value_slot(a) + 1 and h_comes_first(a):
                     divide_by_row_sum(a)
-            if 1 <= n <= ROUNDS:
-                skip_passes(2 * n - 2)
-                skip_passes(2 * n - 1)
+            if c == 9:
+                regroup_v()
+            for r in opening_ln:
+                if r < TILES - 1:
+                    norm_stats(r)
+            for r in closing_ln:
+                norm_centre(r)
+            if c % ROUND_CHUNKS == 1:
+                for a in at(c, 0):
+                    score_matmul(a, 0)
+                    score_matmul(a, 1)
+                if c == 11:
+                    spread_gain_shift()
+                for a in range(TILES):
+                    if c == value_slot(a):
+                        value_passes(a)
+                multiply((c - 3, c - 2))
+            if not last and c % ROUND_CHUNKS == 1 and c // ROUND_CHUNKS + LOAD_AHEAD < ROUNDS:
+                load_round(c // ROUND_CHUNKS + LOAD_AHEAD)
+        multiply((CHUNKS - 2, CHUNKS - 1))
+        for step in (add_streams, norm_stats, norm_moments, norm_centre, norm_finish):
+            step(TILES - 1)

@@ -92,8 +92,11 @@ def tile_spatialprocessor_pa_k_kernel(
         def value_slot(a):
             return first_slot(a) + 10
 
+        def mx_chunks(c):
+            return () if c < 5 else range(c - 5, c - 3) if c < 9 else range(4, 8) if c == 9 else range(c - 3, c - 1)
+
         def skip_taken(r):
-            return CHUNKS_PER_TILE * r + 6
+            return 1 + min(c for c in range(1, CHUNKS + 2, ROUND_CHUNKS) if CHUNKS_PER_TILE * (r + 1) - 1 in mx_chunks(c))
 
         def h_comes_first(r):
             return value_slot(r) + 2 <= skip_taken(r)
@@ -163,17 +166,24 @@ def tile_spatialprocessor_pa_k_kernel(
         load_chunk(pieces=2)
         load_q_and_k()
         load_chunk()
-        load_round(1)
+        load_adj_tile()
+        load_chunk()
+        load_chunk()
+        load_gain_shift()
+        load_adj_tile()
+        load_chunk()
+        load_chunk()
         load_w_scales()
         load_w_codes(0)
         load_w_codes(1)
-        load_round(2)
+        load_adj_tile()
+        load_chunk()
+        load_chunk()
         load_w_codes(2)
         load_w_codes(3)
-        load_round(3)
-        load_round(4)
+        load_chunk()
+        load_chunk()
         load_v()
-        load_gain_shift()
         for n in range(5, LOAD_AHEAD):
             load_round(n)
 
@@ -447,7 +457,7 @@ def tile_spatialprocessor_pa_k_kernel(
             for a in range(TILES):
                 if c == value_slot(a) + 1 and h_comes_first(a):
                     divide_by_row_sum(a)
-            if c == 9:
+            if c == 10:
                 regroup_v()
             for r in opening_ln:
                 if r < TILES - 1:
@@ -458,14 +468,14 @@ def tile_spatialprocessor_pa_k_kernel(
                 for a in at(c, 0):
                     score_matmul(a, 0)
                     score_matmul(a, 1)
-                if c == 11:
+                if c == 5:
                     spread_gain_shift()
                 for a in range(TILES):
                     if c == value_slot(a):
                         value_passes(a)
-                multiply((c - 3, c - 2))
+                multiply(mx_chunks(c))
             if not last and c % ROUND_CHUNKS == 1 and c // ROUND_CHUNKS + LOAD_AHEAD < ROUNDS:
                 load_round(c // ROUND_CHUNKS + LOAD_AHEAD)
-        multiply((CHUNKS - 2, CHUNKS - 1))
+        multiply(mx_chunks(CHUNKS + 1))
         for step in (add_streams, norm_stats, norm_moments, norm_centre, norm_finish):
             step(TILES - 1)

@@ -84,7 +84,7 @@ def tile_spatialprocessor_pa_k_kernel(
         nc.vector.memset(ones[:], 1.0)
 
         def first_slot(a):
-            return 2 * (a * LAST_ATTENTION_ROUND // (TILES - 1)) + 1
+            return 2 * (max(a, (5 * a + 1) // 3 - 2)) + 1
 
         def at(c, stage):
             return [a for a in range(TILES) if first_slot(a) + stage == c]
@@ -179,6 +179,7 @@ def tile_spatialprocessor_pa_k_kernel(
         load_adj_tile()
         load_chunk()
         load_chunk()
+        load_adj_tile()
         load_w_codes(2)
         load_w_codes(3)
         load_chunk()
@@ -424,6 +425,8 @@ def tile_spatialprocessor_pa_k_kernel(
         for c in range(CHUNKS + 1):
             last = c == CHUNKS
             opening_ln, closing_ln, finishing_ln = norm_tiles(c), norm_tiles(c - 1), norm_tiles(c - 2)
+            if c >= CHUNKS - 1:
+                closing_ln, finishing_ln = [], []
             for r in range(TILES):
                 if c == skip_taken(r) and not h_comes_first(r):
                     take_skip(r)
@@ -477,5 +480,11 @@ def tile_spatialprocessor_pa_k_kernel(
             if not last and c % ROUND_CHUNKS == 1 and c // ROUND_CHUNKS + LOAD_AHEAD < ROUNDS:
                 load_round(c // ROUND_CHUNKS + LOAD_AHEAD)
         multiply(mx_chunks(CHUNKS + 1))
-        for step in (add_streams, norm_stats, norm_moments, norm_centre, norm_finish):
-            step(TILES - 1)
+        norm_moments(TILES - 2)
+        add_streams(TILES - 1)
+        norm_centre(TILES - 2)
+        norm_stats(TILES - 1)
+        norm_moments(TILES - 1)
+        norm_centre(TILES - 1)
+        norm_finish(TILES - 2)
+        norm_finish(TILES - 1)

@@ -62,6 +62,7 @@ def tile_spatialprocessor_pa_k_kernel(
         att_pool = ctx.enter_context(tc.tile_pool(name="attention", bufs=3))
         column_pool = ctx.enter_context(tc.tile_pool(name="columns", bufs=4))
         norm_pool = ctx.enter_context(tc.tile_pool(name="norm", bufs=3))
+        split_pool = ctx.enter_context(tc.tile_pool(name="split", bufs=2))
         result_pool = ctx.enter_context(tc.tile_pool(name="result", bufs=TILES))
         flip_psum = ctx.enter_context(tc.psum_pool(name="flip", bufs=4))
         misc_psum = ctx.enter_context(tc.psum_pool(name="misc", bufs=2))
@@ -93,7 +94,7 @@ def tile_spatialprocessor_pa_k_kernel(
             return first_slot(a) + 10
 
         def mx_chunks(c):
-            return () if c < 5 else range(c - 5, c - 3) if c < 9 else range(4, 8) if c == 9 else range(c - 3, c - 1)
+            return () if c < 7 else range(c - 7, c - 5) if c < 11 else range(4, 8) if c == 11 else range(8, 12) if c == 13 else range(c - 3, c - 1)
 
         def skip_taken(r):
             return 1 + min(c for c in range(1, CHUNKS + 2, ROUND_CHUNKS) if CHUNKS_PER_TILE * (r + 1) - 1 in mx_chunks(c))
@@ -169,23 +170,25 @@ def tile_spatialprocessor_pa_k_kernel(
         load_adj_tile()
         load_chunk()
         load_chunk()
+        load_adj_tile()
         load_gain_shift()
+        load_chunk()
+        load_chunk()
         load_adj_tile()
         load_chunk()
+        load_chunk()
+        load_adj_tile()
         load_chunk()
         load_w_scales()
         load_w_codes(0)
         load_w_codes(1)
-        load_adj_tile()
         load_chunk()
         load_chunk()
-        load_adj_tile()
         load_w_codes(2)
         load_w_codes(3)
         load_chunk()
-        load_chunk()
         load_v()
-        for n in range(5, LOAD_AHEAD):
+        for n in range(6, LOAD_AHEAD):
             load_round(n)
 
         gain_shift = keep.tile([P, 2 * D], F32)
@@ -316,6 +319,14 @@ def tile_spatialprocessor_pa_k_kernel(
         skip_banks = {}
         skip_rows = {}
 
+        split_words = {}
+
+        def split_x(c):
+            split_words[c] = split_pool.tile([P, CHUNK_PASSES, 2, P], F32, name="split_words")
+            nc.vector.tensor_copy(
+                out=split_words[c][:], in_=x_chunks[c][:].bitcast(F32).rearrange("p (g w u) -> p g u w", g=CHUNK_PASSES, u=2)
+            )
+
         def flip_x(c, vector_copies=()):
             words = x_chunks[c][:].bitcast(F32)
             x_grouped[c] = grouped_pool.tile([P, CHUNK_PASSES, P, PACK], BF16, name="x_grouped", align_bytes=64)
@@ -327,7 +338,8 @@ def tile_spatialprocessor_pa_k_kernel(
                     for u in range(2):
                         nc.tensor.transpose(
                             bank[:, g, u, :],
-                            words[:, start_word + u : start_word + K_PASS // 2 : 2],
+                            split_words[c][:, first + g, u, :] if c in split_words
+                            else words[:, start_word + u : start_word + K_PASS // 2 : 2],
                             ident_f32[:],
                         )
                 copy = nc.vector.tensor_copy if first in vector_copies else nc.scalar.copy
@@ -442,9 +454,9 @@ def tile_spatialprocessor_pa_k_kernel(
             for a in at(c, 1):
                 mask_scores(a, 0)
                 mask_scores(a, 1)
-            for a in at(c, 3):
+            for a in at(c, 2):
                 row_maximum(a)
-            for a in at(c, 8):
+            for a in at(c, 7):
                 quantise_e(a)
             for r in finishing_ln:
                 norm_finish(r)
@@ -467,6 +479,8 @@ def tile_spatialprocessor_pa_k_kernel(
                     norm_stats(r)
             for r in closing_ln:
                 norm_centre(r)
+            if c + 4 in (28,30):
+                split_x(c + 4)
             if c % ROUND_CHUNKS == 1:
                 for a in at(c, 0):
                     score_matmul(a, 0)

@@ -35,6 +35,8 @@ ROUND_CHUNKS = 2
 ROUNDS = CHUNKS // ROUND_CHUNKS
 ROUNDS_PER_TILE = ROUNDS // TILES
 LAST_ATTENTION_ROUND = 10
+SCALE_GROUPS = ((0, 1, 2, 3), (4, 5))
+FIRST_FINISH = 22
 LOAD_AHEAD = 12
 
 SCALE = 1.0 / math.sqrt(D)
@@ -63,6 +65,7 @@ def tile_spatialprocessor_pa_k_kernel(
         column_pool = ctx.enter_context(tc.tile_pool(name="columns", bufs=4))
         norm_pool = ctx.enter_context(tc.tile_pool(name="norm", bufs=3))
         split_pool = ctx.enter_context(tc.tile_pool(name="split", bufs=2))
+        y_pool = ctx.enter_context(tc.tile_pool(name="y", bufs=TILES))
         result_pool = ctx.enter_context(tc.tile_pool(name="result", bufs=TILES))
         flip_psum = ctx.enter_context(tc.psum_pool(name="flip", bufs=4))
         misc_psum = ctx.enter_context(tc.psum_pool(name="misc", bufs=2))
@@ -73,10 +76,10 @@ def tile_spatialprocessor_pa_k_kernel(
         masks.make_identity(nc, ident_f32[:])
         ident_bf = keep.tile([P, P], BF16)
         masks.make_identity(nc, ident_bf[:])
-        neg_half = keep.tile([P, 1], F32)
+        neg_half = keep.tile([P, TILES], F32)
         nc.vector.memset(neg_half[:], -0.5)
         table_warm = keep.tile([P, 1], F32)
-        nc.scalar.activation(out=table_warm[:], in_=neg_half[:], func=ACT.Exp)
+        nc.scalar.activation(out=table_warm[:], in_=neg_half[:, 0:1], func=ACT.Exp)
         w_planes = keep.tile([P, SKIP_PASSES, D], U8, align_bytes=64)
         nc.vector.memset(w_planes[:].bitcast(I32), 0)
         gain_shift_rows = keep.tile([P, 2 * D], BF16)
@@ -102,8 +105,11 @@ def tile_spatialprocessor_pa_k_kernel(
         def h_comes_first(r):
             return value_slot(r) + 2 <= skip_taken(r)
 
+        def norm_slot(r):
+            return max(skip_taken(r), value_slot(r) + 1)
+
         def norm_tiles(c):
-            return [r for r in range(TILES) if max(skip_taken(r), value_slot(r) + 1) == c]
+            return [r for r in range(TILES) if norm_slot(r) == c]
 
         adj_tiles = []
         x_chunks = []
@@ -376,9 +382,10 @@ def tile_spatialprocessor_pa_k_kernel(
 
         y_rows = {}
         stats = {}
-        mean_var = {}
         centred = {}
-        inv_std = {}
+        mean_var = keep.tile([P, TILES, 2], F32)
+        var_eps = keep.tile([P, TILES], F32)
+        inv_std = keep.tile([P, TILES], F32)
 
         h_rows = {}
 
@@ -391,7 +398,7 @@ def tile_spatialprocessor_pa_k_kernel(
             nc.scalar.copy(out=skip_rows[r][:], in_=skip_banks[r][:])
 
         def add_streams(r):
-            y_rows[r] = norm_pool.tile([P, D], F32, name="y")
+            y_rows[r] = y_pool.tile([P, D], F32, name="y")
             if h_comes_first(r):
                 nc.vector.tensor_tensor(out=y_rows[r][:], in0=skip_banks[r][:], in1=h_rows[r][:], op=ALU.add)
                 return
@@ -405,29 +412,41 @@ def tile_spatialprocessor_pa_k_kernel(
             nc.vector.bn_stats(out=stats[r][:], in_=y_rows[r][:])
 
         def norm_moments(r):
-            mean_var[r] = column_pool.tile([P, 2], F32, name="mean_var")
-            nc.vector.bn_aggr(out=mean_var[r][:], in_=stats[r][:])
-            var_eps = column_pool.tile([P, 1], F32, name="var_eps")
-            nc.gpsimd.tensor_scalar(
-                out=var_eps[:], in0=mean_var[r][:, 1:2], scalar1=LN_EPS, scalar2=None, op0=ALU.add
+            nc.vector.bn_aggr(out=mean_var[:, r], in_=stats[r][:])
+
+        def norm_scales(tiles):
+            columns = slice(tiles[0], tiles[-1] + 1)
+            nc.vector.tensor_scalar(
+                out=var_eps[:, columns], in0=mean_var[:, columns, 1], scalar1=LN_EPS, scalar2=None, op0=ALU.add
             )
-            inv_std[r] = column_pool.tile([P, 1], F32, name="inv_std")
-            nc.gpsimd.tensor_tensor(out=inv_std[r][:], in0=var_eps[:], in1=neg_half[:], op=ALU.pow)
+            nc.gpsimd.tensor_tensor(
+                out=inv_std[:, columns], in0=var_eps[:, columns], in1=neg_half[:, columns], op=ALU.pow
+            )
 
         def norm_centre(r):
             centred[r] = norm_pool.tile([P, D], F32, name="centred")
             nc.vector.scalar_tensor_tensor(
-                out=centred[r][:], in0=y_rows[r][:], scalar=mean_var[r][:, 0:1], in1=gain,
+                out=centred[r][:], in0=y_rows[r][:], scalar=mean_var[:, r, 0:1], in1=gain,
                 op0=ALU.subtract, op1=ALU.mult,
             )
 
         def norm_finish(r):
             result = result_pool.tile([P, D], F32, name="result")
             nc.vector.scalar_tensor_tensor(
-                out=result[:], in0=centred[r][:], scalar=inv_std[r][:], in1=shift,
+                out=result[:], in0=centred[r][:], scalar=inv_std[:, r : r + 1], in1=shift,
                 op0=ALU.mult, op1=ALU.add,
             )
             nc.sync.dma_start(out=out_tiles[r], in_=result[:])
+
+        def scales_slot(tiles):
+            return max(norm_slot(r) for r in tiles) + 1
+
+        def centre_slot(r):
+            return max(FIRST_FINISH + r, norm_slot(r) + 1)
+
+        def finish_slot(r):
+            tiles = [t for t in SCALE_GROUPS if r in t][0]
+            return max(centre_slot(r) + 1, scales_slot(tiles) + 2 + r - tiles[0])
 
         def multiply(chunks):
             for c in chunks:
@@ -436,9 +455,9 @@ def tile_spatialprocessor_pa_k_kernel(
 
         for c in range(CHUNKS + 1):
             last = c == CHUNKS
-            opening_ln, closing_ln, finishing_ln = norm_tiles(c), norm_tiles(c - 1), norm_tiles(c - 2)
+            opening_ln, closing_ln = norm_tiles(c), norm_tiles(c - 1)
             if c >= CHUNKS - 1:
-                closing_ln, finishing_ln = [], []
+                closing_ln = []
             for r in range(TILES):
                 if c == skip_taken(r) and not h_comes_first(r):
                     take_skip(r)
@@ -458,8 +477,9 @@ def tile_spatialprocessor_pa_k_kernel(
                 row_maximum(a)
             for a in at(c, 7):
                 quantise_e(a)
-            for r in finishing_ln:
-                norm_finish(r)
+            for r in range(TILES - 2):
+                if c == finish_slot(r):
+                    norm_finish(r)
             if not last:
                 flip_x(c, ())
             if c == 0:
@@ -477,8 +497,12 @@ def tile_spatialprocessor_pa_k_kernel(
             for r in opening_ln:
                 if r < TILES - 1:
                     norm_stats(r)
-            for r in closing_ln:
-                norm_centre(r)
+            for tiles in SCALE_GROUPS:
+                if c == scales_slot(tiles):
+                    norm_scales(tiles)
+            for r in range(TILES - 2):
+                if c == centre_slot(r):
+                    norm_centre(r)
             if c + 4 in (28,30):
                 split_x(c + 4)
             if c % ROUND_CHUNKS == 1:
@@ -496,9 +520,11 @@ def tile_spatialprocessor_pa_k_kernel(
         multiply(mx_chunks(CHUNKS + 1))
         norm_moments(TILES - 2)
         add_streams(TILES - 1)
-        norm_centre(TILES - 2)
+        norm_scales([TILES - 2])
         norm_stats(TILES - 1)
+        norm_centre(TILES - 2)
         norm_moments(TILES - 1)
-        norm_centre(TILES - 1)
         norm_finish(TILES - 2)
+        norm_scales([TILES - 1])
+        norm_centre(TILES - 1)
         norm_finish(TILES - 1)

@@ -78,6 +78,8 @@ def tile_spatialprocessor_pa_k_kernel(
         masks.make_identity(nc, ident_bf[:])
         neg_half = keep.tile([P, TILES], F32)
         nc.vector.memset(neg_half[:], -0.5)
+        neg_one = keep.tile([P, 1], F32)
+        nc.vector.memset(neg_one[:], -1.0)
         table_warm = keep.tile([P, 1], F32)
         nc.scalar.activation(out=table_warm[:], in_=neg_half[:, 0:1], func=ACT.Exp)
         w_planes = keep.tile([P, SKIP_PASSES, D], U8, align_bytes=64)
@@ -303,7 +305,7 @@ def tile_spatialprocessor_pa_k_kernel(
                 in_=e_grouped[a][:].rearrange("p c i t -> p (c i t)"),
             )
             inv_sum = column_pool.tile([P, 1], F32, name="inv_sum")
-            nc.vector.reciprocal(out=inv_sum[:], in_=row_sums[a][:])
+            nc.gpsimd.tensor_tensor(out=inv_sum[:], in0=row_sums[a][:], in1=neg_one[:], op=ALU.pow)
             e_operands[a] = (codes, planes, inv_sum)
 
         def value_passes(a):

@@ -57,7 +57,7 @@ def tile_spatialprocessor_pa_k_kernel(
     with ExitStack() as ctx:
         ctx.enter_context(tc.manual_schedule())
         keep = ctx.enter_context(tc.tile_pool(name="keep", bufs=1))
-        x_pool = ctx.enter_context(tc.tile_pool(name="x", bufs=LOAD_AHEAD * ROUND_CHUNKS))
+        x_pool = ctx.enter_context(tc.tile_pool(name="x", bufs=LOAD_AHEAD))
         adj_pool = ctx.enter_context(tc.tile_pool(name="adj", bufs=TILES))
         grouped_pool = ctx.enter_context(tc.tile_pool(name="grouped", bufs=6))
         code_pool = ctx.enter_context(tc.tile_pool(name="codes", bufs=8))
@@ -114,6 +114,7 @@ def tile_spatialprocessor_pa_k_kernel(
             return [r for r in range(TILES) if norm_slot(r) == c]
 
         adj_tiles = []
+        x_rounds = []
         x_chunks = []
 
         def load_adj_tile():
@@ -122,22 +123,32 @@ def tile_spatialprocessor_pa_k_kernel(
             nc.sync.dma_start(out=adj_tile[:], in_=adj_rows[a])
             adj_tiles.append(adj_tile)
 
+        def new_round():
+            x_rounds.append(x_pool.tile([P, ROUND_CHUNKS * CHUNK_K], BF16, name="x_round"))
+
+        def round_rows(n):
+            r, half = divmod(n, ROUNDS_PER_TILE)
+            return x_tiles[r][:, ROUND_CHUNKS * CHUNK_K * half : ROUND_CHUNKS * CHUNK_K * (half + 1)]
+
+        def halves(x_round):
+            return [x_round[:, CHUNK_K * i : CHUNK_K * (i + 1)] for i in range(ROUND_CHUNKS)]
+
         def load_chunk(pieces=1):
-            r, part = divmod(len(x_chunks), CHUNKS_PER_TILE)
-            x_chunk = x_pool.tile([P, CHUNK_K], BF16, name="x_chunk")
+            n, i = divmod(len(x_chunks), ROUND_CHUNKS)
+            if i == 0:
+                new_round()
             width = CHUNK_K // pieces
-            for i in range(pieces):
-                nc.sync.dma_start(
-                    out=x_chunk[:, width * i : width * (i + 1)],
-                    in_=x_tiles[r][:, CHUNK_K * part + width * i : CHUNK_K * part + width * (i + 1)],
-                )
-            x_chunks.append(x_chunk)
+            for first in range(CHUNK_K * i, CHUNK_K * (i + 1), width):
+                columns = slice(first, first + width)
+                nc.sync.dma_start(out=x_rounds[n][:, columns], in_=round_rows(n)[:, columns])
+            x_chunks.append(halves(x_rounds[n])[i])
 
         def load_round(n):
             for _ in at(2 * n, 1):
                 load_adj_tile()
-            for _ in range(ROUND_CHUNKS):
-                load_chunk()
+            new_round()
+            nc.sync.dma_start(out=x_rounds[-1][:], in_=round_rows(n))
+            x_chunks.extend(halves(x_rounds[-1]))
 
         w_codes = keep.tile([P, SKIP_PASSES, D], U32, align_bytes=64)
         w_words = proj_w_words.bitcast(I32).rearrange("g p n o -> p g (n o)")
@@ -172,7 +183,7 @@ def tile_spatialprocessor_pa_k_kernel(
             nc.sync.dma_start(out=gain_shift_rows[0:1, 0:D], in_=ln_g.unsqueeze(0))
             nc.sync.dma_start(out=gain_shift_rows[0:1, D : 2 * D], in_=ln_b.unsqueeze(0))
 
-        load_chunk(pieces=2)
+        load_chunk(pieces=4)
         load_q_and_k()
         load_chunk()
         load_adj_tile()
@@ -332,11 +343,11 @@ def tile_spatialprocessor_pa_k_kernel(
         def split_x(c):
             split_words[c] = split_pool.tile([P, CHUNK_PASSES, 2, P], F32, name="split_words")
             nc.vector.tensor_copy(
-                out=split_words[c][:], in_=x_chunks[c][:].bitcast(F32).rearrange("p (g w u) -> p g u w", g=CHUNK_PASSES, u=2)
+                out=split_words[c][:], in_=x_chunks[c].bitcast(F32).rearrange("p (g w u) -> p g u w", g=CHUNK_PASSES, u=2)
             )
 
         def flip_x(c, vector_copies=()):
-            words = x_chunks[c][:].bitcast(F32)
+            words = x_chunks[c].bitcast(F32)
             x_grouped[c] = grouped_pool.tile([P, CHUNK_PASSES, P, PACK], BF16, name="x_grouped", align_bytes=64)
             grouped_words = x_grouped[c][:].bitcast(F32)
             for first in range(0, CHUNK_PASSES, 2):

from contextlib import ExitStack
import math

import concourse.masks as masks
import concourse.mybir as mybir

F32 = mybir.dt.float32
BF16 = mybir.dt.bfloat16
I32 = mybir.dt.int32
U32 = mybir.dt.uint32
U8 = mybir.dt.uint8
FP8X4 = mybir.dt.float8_e4m3fn_x4
ALU = mybir.AluOpType
ACT = mybir.ActivationFunctionType
AXIS_X = mybir.AxisListType.X

P = 128
PACK = 4
K_PASS = P * PACK
NODES = 1024
D = 128
F_IN = 8192
TILES = NODES // P
KEY_PASSES = NODES // K_PASS
SKIP_PASSES = F_IN // K_PASS
BANK = 512
SCORE_HALVES = NODES // BANK
SCORE_PART = BANK // 2

CHUNK_PASSES = 4
CHUNK_K = CHUNK_PASSES * K_PASS
CHUNKS_PER_TILE = F_IN // CHUNK_K
CHUNKS = TILES * CHUNKS_PER_TILE
ROUND_CHUNKS = 2
ROUNDS = CHUNKS // ROUND_CHUNKS
ROUNDS_PER_TILE = ROUNDS // TILES
LAST_ATTENTION_ROUND = 10
SCALE_GROUPS = ((0, 1, 2, 3), (4, 5))
FIRST_FINISH = 22
LOAD_AHEAD = 12

SCALE = 1.0 / math.sqrt(D)
PENALTY = 2.0**34
LN_EPS = 1e-3

FLOPS = 2 * NODES * NODES * D * 2 + 2 * NODES * F_IN * D


def tile_spatialprocessor_pa_k_kernel(
    tc, q2, k2, v2, adj, x, proj_w_words, proj_w_scales, ln_g, ln_b, out
):
    nc = tc.nc
    x_tiles = x.rearrange("b (p t) k -> (b t) p k", t=TILES)
    adj_rows = adj.rearrange("(p t) j -> t p j", t=TILES)
    out_tiles = out.rearrange("b (p t) d -> (b t) p d", t=TILES)

    with ExitStack() as ctx:
        ctx.enter_context(tc.manual_schedule())
        keep = ctx.enter_context(tc.tile_pool(name="keep", bufs=1))
        x_pool = ctx.enter_context(tc.tile_pool(name="x", bufs=LOAD_AHEAD))
        adj_pool = ctx.enter_context(tc.tile_pool(name="adj", bufs=TILES))
        grouped_pool = ctx.enter_context(tc.tile_pool(name="grouped", bufs=6))
        code_pool = ctx.enter_context(tc.tile_pool(name="codes", bufs=8))
        att_pool = ctx.enter_context(tc.tile_pool(name="attention", bufs=3))
        column_pool = ctx.enter_context(tc.tile_pool(name="columns", bufs=4))
        norm_pool = ctx.enter_context(tc.tile_pool(name="norm", bufs=3))
        split_pool = ctx.enter_context(tc.tile_pool(name="split", bufs=2))
        y_pool = ctx.enter_context(tc.tile_pool(name="y", bufs=TILES))
        result_pool = ctx.enter_context(tc.tile_pool(name="result", bufs=TILES))
        flip_psum = ctx.enter_context(tc.psum_pool(name="flip", bufs=4))
        misc_psum = ctx.enter_context(tc.psum_pool(name="misc", bufs=2))
        h_psum = ctx.enter_context(tc.psum_pool(name="h", bufs=1))
        skip_psum = ctx.enter_context(tc.psum_pool(name="skip", bufs=1))

        ident_f32 = keep.tile([P, P], F32)
        masks.make_identity(nc, ident_f32[:])
        ident_bf = keep.tile([P, P], BF16)
        masks.make_identity(nc, ident_bf[:])
        neg_half = keep.tile([P, TILES], F32)
        nc.vector.memset(neg_half[:], -0.5)
        neg_one = keep.tile([P, 1], F32)
        nc.vector.memset(neg_one[:], -1.0)
        table_warm = keep.tile([P, 1], F32)
        nc.scalar.activation(out=table_warm[:], in_=neg_half[:, 0:1], func=ACT.Exp)
        w_planes = keep.tile([P, SKIP_PASSES, D], U8, align_bytes=64)
        nc.vector.memset(w_planes[:].bitcast(I32), 0)
        gain_shift_rows = keep.tile([P, 2 * D], BF16)
        nc.vector.memset(gain_shift_rows[:].bitcast(I32), 0)
        ones = keep.tile([P, P], BF16)
        nc.vector.memset(ones[:], 1.0)

        def first_slot(a):
            return 2 * (max(a, (5 * a + 1) // 3 - 2)) + 1

        def at(c, stage):
            return [a for a in range(TILES) if first_slot(a) + stage == c]

        def value_slot(a):
            return first_slot(a) + 10

        def mx_chunks(c):
            return () if c < 7 else range(c - 7, c - 5) if c < 11 else range(4, 8) if c == 11 else range(8, 12) if c == 13 else range(c - 3, c - 1)

        def skip_taken(r):
            return 1 + min(c for c in range(1, CHUNKS + 2, ROUND_CHUNKS) if CHUNKS_PER_TILE * (r + 1) - 1 in mx_chunks(c))

        def h_comes_first(r):
            return value_slot(r) + 2 <= skip_taken(r)

        def norm_slot(r):
            return max(skip_taken(r), value_slot(r) + 1)

        def norm_tiles(c):
            return [r for r in range(TILES) if norm_slot(r) == c]

        adj_tiles = []
        x_rounds = []
        x_chunks = []

        def load_adj_tile():
            a = len(adj_tiles)
            adj_tile = adj_pool.tile([P, NODES], BF16, name="adj_tile")
            nc.sync.dma_start(out=adj_tile[:], in_=adj_rows[a])
            adj_tiles.append(adj_tile)

        def new_round():
            x_rounds.append(x_pool.tile([P, ROUND_CHUNKS * CHUNK_K], BF16, name="x_round"))

        def round_rows(n):
            r, half = divmod(n, ROUNDS_PER_TILE)
            return x_tiles[r][:, ROUND_CHUNKS * CHUNK_K * half : ROUND_CHUNKS * CHUNK_K * (half + 1)]

        def halves(x_round):
            return [x_round[:, CHUNK_K * i : CHUNK_K * (i + 1)] for i in range(ROUND_CHUNKS)]

        def load_chunk(pieces=1):
            n, i = divmod(len(x_chunks), ROUND_CHUNKS)
            if i == 0:
                new_round()
            width = CHUNK_K // pieces
            for first in range(CHUNK_K * i, CHUNK_K * (i + 1), width):
                columns = slice(first, first + width)
                nc.sync.dma_start(out=x_rounds[n][:, columns], in_=round_rows(n)[:, columns])
            x_chunks.append(halves(x_rounds[n])[i])

        def load_round(n):
            for _ in at(2 * n, 1):
                load_adj_tile()
            new_round()
            nc.sync.dma_start(out=x_rounds[-1][:], in_=round_rows(n))
            x_chunks.extend(halves(x_rounds[-1]))

        w_codes = keep.tile([P, SKIP_PASSES, D], U32, align_bytes=64)
        w_words = proj_w_words.bitcast(I32).rearrange("g p n o -> p g (n o)")
        w_scale_words = proj_w_scales.bitcast(I32)

        def load_w_scales():
            for quadrant in range(4):
                nc.sync.dma_start(
                    out=w_planes[32 * quadrant : 32 * quadrant + 4, :, :].bitcast(I32),
                    in_=w_scale_words[:, 4 * quadrant : 4 * quadrant + 4, :].rearrange("g r n -> r g n"),
                )

        def load_w_codes(part):
            passes = slice(CHUNK_PASSES * part, CHUNK_PASSES * (part + 1))
            nc.sync.dma_start(out=w_codes[:, passes, :].bitcast(I32), in_=w_words[:, passes, :])

        q_rows = keep.tile([P, TILES, D], BF16)
        k_rows = keep.tile([P, TILES, D], BF16)
        v_rows = keep.tile([P, KEY_PASSES, 2, 2, D], BF16)

        def load_q_and_k():
            nc.sync.dma_start(out=q_rows[:], in_=q2.rearrange("b (p t) d -> p (b t) d", t=TILES))
            nc.sync.dma_start(out=k_rows[:], in_=k2.rearrange("b (p t) d -> p (b t) d", t=TILES))

        def load_v():
            nc.sync.dma_start(
                out=v_rows[:].rearrange("p c u e d -> p (c u) (e d)"),
                in_=v2.rearrange("b (s p e) d -> p (b s) (e d)", p=P, e=2),
            )

        def load_gain_shift():
            nc.sync.dma_start(out=gain_shift_rows[0:1, 0:D], in_=ln_g.unsqueeze(0))
            nc.sync.dma_start(out=gain_shift_rows[0:1, D : 2 * D], in_=ln_b.unsqueeze(0))

        load_chunk(pieces=4)
        load_q_and_k()
        load_chunk()
        load_adj_tile()
        load_chunk()
        load_chunk()
        load_adj_tile()
        load_gain_shift()
        load_chunk()
        load_chunk()
        load_adj_tile()
        load_chunk()
        load_chunk()
        load_adj_tile()
        load_chunk()
        load_w_scales()
        load_w_codes(0)
        load_w_codes(1)
        load_chunk()
        load_chunk()
        load_w_codes(2)
        load_w_codes(3)
        load_chunk()
        load_v()
        for n in range(6, LOAD_AHEAD):
            load_round(n)

        gain_shift = keep.tile([P, 2 * D], F32)
        gain = gain_shift[:, 0:D]
        shift = gain_shift[:, D : 2 * D]

        def spread_gain_shift():
            bank = h_psum.tile([P, 2 * D], F32, name="gain_shift_bank", tag="h")
            nc.tensor.matmul(out=bank[:], lhsT=ones[:], rhs=gain_shift_rows[:], start=True, stop=True)
            nc.scalar.copy(out=gain_shift[:], in_=bank[:])

        q_cols = keep.tile([P, TILES, P], BF16)
        k_cols = keep.tile([P, NODES], BF16)

        def flip_q_and_k():
            q_bank = misc_psum.tile([P, TILES, P], BF16, name="q_bank", tag="misc")
            for t in range(TILES):
                nc.tensor.transpose(q_bank[:, t, :], q_rows[:, t, :], ident_bf[:])
            nc.vector.tensor_scalar(
                out=q_cols[:], in0=q_bank[:], scalar1=1.0 / PENALTY, scalar2=None, op0=ALU.mult
            )
            k_bank = misc_psum.tile([P, TILES, P], BF16, name="k_bank", tag="misc")
            for t in range(TILES):
                nc.tensor.transpose(k_bank[:, t, :], k_rows[:, t, :], ident_bf[:])
            nc.vector.tensor_copy(
                out=k_cols[:].rearrange("d (p t) -> d p t", t=TILES), in_=k_bank[:].rearrange("d t p -> d p t")
            )

        v_codes = keep.tile([P, KEY_PASSES * D], U32, align_bytes=64)
        v_planes = keep.tile([P, KEY_PASSES * D], U8, align_bytes=64)
        v_grouped = keep.tile([P, KEY_PASSES, D, PACK], BF16, align_bytes=64)

        def regroup_v():
            for c in range(KEY_PASSES):
                nc.vector.tensor_copy(
                    out=v_grouped[:, c], in_=v_rows[:, c].rearrange("p u e d -> p d (u e)")
                )

        def quantise_v():
            nc.vector.quantize_mx(
                out=v_codes[:].bitcast(FP8X4),
                scales=v_planes[:],
                in_=v_grouped[:].rearrange("p c d t -> p (c d t)"),
            )

        score_banks = {}
        neg_scores = {}
        neg_max = {}
        e_rows = {}
        row_sums = {}
        e_banks = {}
        e_grouped = {}
        e_operands = {}
        h_banks = {}

        def score_matmul(a, half):
            bank = misc_psum.tile([P, BANK], F32, name="score_bank", tag="misc")
            keys = slice(BANK * half, BANK * (half + 1))
            nc.tensor.matmul(out=bank[:], lhsT=q_cols[:, a, :], rhs=k_cols[:, keys], start=True, stop=True)
            score_banks[a, half] = bank

        def mask_scores(a, half):
            if half == 0:
                neg_scores[a] = att_pool.tile([P, NODES], F32, name="neg_scores")
            keys = slice(BANK * half, BANK * (half + 1))
            nc.vector.scalar_tensor_tensor(
                out=neg_scores[a][:, keys], in0=adj_tiles[a][:, keys], scalar=0.0, in1=score_banks[a, half][:],
                op0=ALU.is_equal, op1=ALU.subtract,
            )

        def row_maximum(a):
            neg_max[a] = column_pool.tile([P, 1], F32, name="neg_max")
            nc.vector.tensor_scalar(
                out=neg_scores[a][:], in0=neg_scores[a][:], scalar1=PENALTY * SCALE, scalar2=None,
                op0=ALU.mult, op1=ALU.min, accum_out=neg_max[a][:],
            )

        def exponentials(a):
            e_rows[a] = att_pool.tile([P, NODES], BF16, name="e_rows")
            row_sums[a] = column_pool.tile([P, 1], F32, name="row_sum")
            nc.scalar.activation(
                out=e_rows[a][:], in_=neg_scores[a][:], func=ACT.Exp, bias=neg_max[a][:], scale=-1.0,
                accum_out=row_sums[a][:],
            )

        def flip_e(a):
            words = e_rows[a][:].bitcast(F32)
            bank = flip_psum.tile([P, KEY_PASSES, 2, P], F32, name="e_bank", tag="flip")
            for c in range(KEY_PASSES):
                for u in range(2):
                    first = P * (2 * c + u)
                    nc.tensor.transpose(bank[:, c, u, :], words[:, first : first + P], ident_f32[:])
            e_banks[a] = bank

        def regroup_e(a):
            e_grouped[a] = att_pool.tile([P, KEY_PASSES, P, PACK], BF16, name="e_grouped", align_bytes=64)
            nc.scalar.copy(
                out=e_grouped[a][:].bitcast(F32), in_=e_banks[a][:].rearrange("p c u i -> p c i u")
            )

        def quantise_e(a):
            codes = att_pool.tile([P, KEY_PASSES * P], U32, name="e_codes", align_bytes=64)
            planes = att_pool.tile([P, KEY_PASSES * P], U8, name="e_planes", align_bytes=64)
            nc.vector.quantize_mx(
                out=codes[:].bitcast(FP8X4), scales=planes[:],
                in_=e_grouped[a][:].rearrange("p c i t -> p (c i t)"),
            )
            inv_sum = column_pool.tile([P, 1], F32, name="inv_sum")
            nc.gpsimd.tensor_tensor(out=inv_sum[:], in0=row_sums[a][:], in1=neg_one[:], op=ALU.pow)
            e_operands[a] = (codes, planes, inv_sum)

        def value_passes(a):
            codes, planes = e_operands[a][0:2]
            h_banks[a] = h_psum.tile([P, D], F32, name="h_bank", tag="h")
            for c in range(KEY_PASSES):
                nc.tensor.matmul_mx(
                    out=h_banks[a][:],
                    lhsT=codes[:, P * c : P * (c + 1)].bitcast(FP8X4),
                    lhsT_scale=planes[:, P * c : P * (c + 1)],
                    rhs=v_codes[:, D * c : D * (c + 1)].bitcast(FP8X4),
                    rhs_scale=v_planes[:, D * c : D * (c + 1)],
                    start=(c == 0),
                    stop=(c == KEY_PASSES - 1),
                )

        x_grouped = {}
        x_operands = {}
        skip_banks = {}
        skip_rows = {}

        split_words = {}

        def split_x(c):
            split_words[c] = split_pool.tile([P, CHUNK_PASSES, 2, P], F32, name="split_words")
            nc.vector.tensor_copy(
                out=split_words[c][:], in_=x_chunks[c].bitcast(F32).rearrange("p (g w u) -> p g u w", g=CHUNK_PASSES, u=2)
            )

        def flip_x(c, vector_copies=()):
            words = x_chunks[c].bitcast(F32)
            x_grouped[c] = grouped_pool.tile([P, CHUNK_PASSES, P, PACK], BF16, name="x_grouped", align_bytes=64)
            grouped_words = x_grouped[c][:].bitcast(F32)
            for first in range(0, CHUNK_PASSES, 2):
                bank = flip_psum.tile([P, 2, 2, P], F32, name="x_bank", tag="flip")
                for g in range(2):
                    start_word = (K_PASS // 2) * (first + g)
                    for u in range(2):
                        nc.tensor.transpose(
                            bank[:, g, u, :],
                            split_words[c][:, first + g, u, :] if c in split_words
                            else words[:, start_word + u : start_word + K_PASS // 2 : 2],
                            ident_f32[:],
                        )
                copy = nc.vector.tensor_copy if first in vector_copies else nc.scalar.copy
                copy(out=grouped_words[:, first : first + 2], in_=bank[:].rearrange("p g u n -> p g n u"))

        def quantise_x(c, pieces=1):
            codes = code_pool.tile([P, CHUNK_PASSES * P], U32, name="x_codes", align_bytes=64)
            planes = code_pool.tile([P, CHUNK_PASSES * P], U8, name="x_planes", align_bytes=64)
            passes = CHUNK_PASSES // pieces
            for i in range(pieces):
                columns = slice(P * passes * i, P * passes * (i + 1))
                nc.vector.quantize_mx(
                    out=codes[:, columns].bitcast(FP8X4), scales=planes[:, columns],
                    in_=x_grouped[c][:, passes * i : passes * (i + 1)].rearrange("p g n t -> p (g n t)"),
                )
            x_operands[c] = (codes, planes)

        def skip_passes(c):
            r, part = divmod(c, CHUNKS_PER_TILE)
            if part == 0:
                skip_banks[r] = skip_psum.tile([P, D], F32, name="skip_bank", tag="skip")
            codes, planes = x_operands[c]
            for g in range(CHUNK_PASSES):
                w_pass = CHUNK_PASSES * part + g
                nc.tensor.matmul_mx(
                    out=skip_banks[r][:],
                    lhsT=codes[:, P * g : P * (g + 1)].bitcast(FP8X4),
                    lhsT_scale=planes[:, P * g : P * (g + 1)],
                    rhs=w_codes[:, w_pass, :].bitcast(FP8X4),
                    rhs_scale=w_planes[:, w_pass, :],
                    start=(w_pass == 0),
                    stop=(w_pass == SKIP_PASSES - 1),
                )

        y_rows = {}
        stats = {}
        centred = {}
        mean_var = keep.tile([P, TILES, 2], F32)
        var_eps = keep.tile([P, TILES], F32)
        inv_std = keep.tile([P, TILES], F32)

        h_rows = {}

        def divide_by_row_sum(a):
            h_rows[a] = norm_pool.tile([P, D], F32, name="h_rows")
            nc.scalar.activation(out=h_rows[a][:], in_=h_banks[a][:], func=ACT.Copy, scale=e_operands[a][2][:])

        def take_skip(r):
            skip_rows[r] = norm_pool.tile([P, D], F32, name="skip_rows")
            nc.scalar.copy(out=skip_rows[r][:], in_=skip_banks[r][:])

        def add_streams(r):
            y_rows[r] = y_pool.tile([P, D], F32, name="y")
            if h_comes_first(r):
                nc.vector.tensor_tensor(out=y_rows[r][:], in0=skip_banks[r][:], in1=h_rows[r][:], op=ALU.add)
                return
            nc.vector.scalar_tensor_tensor(
                out=y_rows[r][:], in0=h_banks[r][:], scalar=e_operands[r][2][:], in1=skip_rows[r][:],
                op0=ALU.mult, op1=ALU.add,
            )

        def norm_stats(r):
            stats[r] = column_pool.tile([P, 6], F32, name="stats")
            nc.vector.bn_stats(out=stats[r][:], in_=y_rows[r][:])

        def norm_moments(r):
            nc.vector.bn_aggr(out=mean_var[:, r], in_=stats[r][:])

        def norm_scales(tiles):
            columns = slice(tiles[0], tiles[-1] + 1)
            nc.vector.tensor_scalar(
                out=var_eps[:, columns], in0=mean_var[:, columns, 1], scalar1=LN_EPS, scalar2=None, op0=ALU.add
            )
            nc.gpsimd.tensor_tensor(
                out=inv_std[:, columns], in0=var_eps[:, columns], in1=neg_half[:, columns], op=ALU.pow
            )

        def norm_centre(r):
            centred[r] = norm_pool.tile([P, D], F32, name="centred")
            nc.vector.scalar_tensor_tensor(
                out=centred[r][:], in0=y_rows[r][:], scalar=mean_var[:, r, 0:1], in1=gain,
                op0=ALU.subtract, op1=ALU.mult,
            )

        def norm_finish(r):
            result = result_pool.tile([P, D], F32, name="result")
            nc.vector.scalar_tensor_tensor(
                out=result[:], in0=centred[r][:], scalar=inv_std[:, r : r + 1], in1=shift,
                op0=ALU.mult, op1=ALU.add,
            )
            nc.sync.dma_start(out=out_tiles[r], in_=result[:])

        def scales_slot(tiles):
            return max(norm_slot(r) for r in tiles) + 1

        def centre_slot(r):
            return max(FIRST_FINISH + r, norm_slot(r) + 1)

        def finish_slot(r):
            tiles = [t for t in SCALE_GROUPS if r in t][0]
            return max(centre_slot(r) + 1, scales_slot(tiles) + 2 + r - tiles[0])

        def multiply(chunks):
            for c in chunks:
                if 0 <= c < CHUNKS:
                    skip_passes(c)

        for c in range(CHUNKS + 1):
            last = c == CHUNKS
            opening_ln, closing_ln = norm_tiles(c), norm_tiles(c - 1)
            if c >= CHUNKS - 1:
                closing_ln = []
            for r in range(TILES):
                if c == skip_taken(r) and not h_comes_first(r):
                    take_skip(r)
            if c >= 1:
                quantise_x(c - 1, 2 if last else 1)
            if c == 11:
                quantise_v()
            for r in opening_ln:
                if r < TILES - 1:
                    add_streams(r)
            for r in closing_ln:
                norm_moments(r)
            for a in at(c, 1):
                mask_scores(a, 0)
                mask_scores(a, 1)
            for a in at(c, 2):
                row_maximum(a)
            for a in at(c, 7):
                quantise_e(a)
            for r in range(TILES - 2):
                if c == finish_slot(r):
                    norm_finish(r)
            if not last:
                flip_x(c, ())
            if c == 0:
                flip_q_and_k()
            for a in at(c, 6):
                flip_e(a)
                regroup_e(a)
            for a in at(c, 4):
                exponentials(a)
            for a in range(TILES):
                if c == value_slot(a) + 1 and h_comes_first(a):
                    divide_by_row_sum(a)
            if c == 10:
                regroup_v()
            for r in opening_ln:
                if r < TILES - 1:
                    norm_stats(r)
            for tiles in SCALE_GROUPS:
                if c == scales_slot(tiles):
                    norm_scales(tiles)
            for r in range(TILES - 2):
                if c == centre_slot(r):
                    norm_centre(r)
            if c + 4 in (28,30):
                split_x(c + 4)
            if c % ROUND_CHUNKS == 1:
                for a in at(c, 0):
                    score_matmul(a, 0)
                    score_matmul(a, 1)
                if c == 5:
                    spread_gain_shift()
                for a in range(TILES):
                    if c == value_slot(a):
                        value_passes(a)
                multiply(mx_chunks(c))
            if not last and c % ROUND_CHUNKS == 1 and c // ROUND_CHUNKS + LOAD_AHEAD < ROUNDS:
                load_round(c // ROUND_CHUNKS + LOAD_AHEAD)
        multiply(mx_chunks(CHUNKS + 1))
        norm_moments(TILES - 2)
        add_streams(TILES - 1)
        norm_scales([TILES - 2])
        norm_stats(TILES - 1)
        norm_centre(TILES - 2)
        norm_moments(TILES - 1)
        norm_finish(TILES - 2)
        norm_scales([TILES - 1])
        norm_centre(TILES - 1)
        norm_finish(TILES - 1)
